import numpy as np
import ml_dtypes


def mxq(x, axis, fmt="e4m3"):
    dtype, down = {"e4m3": (ml_dtypes.float8_e4m3fn, 7), "e5m2": (ml_dtypes.float8_e5m2, 14)}[fmt]
    v = np.moveaxis(np.asarray(x, np.float32).astype(ml_dtypes.bfloat16).astype(np.float64), axis, -1)
    blocks = v.reshape(v.shape[:-1] + (-1, 32))
    amax = np.abs(blocks).max(-1, keepdims=True)
    byte = np.maximum(np.where(amax > 0, np.frexp(amax)[1] - 1 + 127, 0) - down, 1)
    scale = np.exp2(byte - 127.0)
    codes = (blocks / scale).astype(np.float32).astype(dtype).astype(np.float64)
    return np.moveaxis((codes * scale).reshape(v.shape), -1, axis)


WIDE = False


def mx_kscale(k):
    if not WIDE:
        return np.ones(k)
    levels = np.array([10, -10, 5, -5, 0])
    a = np.random.permutation(np.resize(levels, k // 512 * 4)).reshape(k // 512, 4)
    idx = np.arange(k)
    return np.exp2(a[idx // 512, idx % 128 // 32])


BF16 = ml_dtypes.bfloat16


def bf(x):
    return np.asarray(x, np.float32).astype(BF16)


def f64(x):
    return np.asarray(x).astype(np.float64)


BS, BLOCK, HID, GAP, G = 4096, 512, 512, 64, 2


def elu(v):
    return np.where(v > 0.0, v, np.exp(np.minimum(v, 0.0)) - 1.0)


def setup_inputs():
    s = mx_kscale(BLOCK)
    s = s / s.max()
    return {"x_blocks": bf((np.random.standard_normal((BS, G, BLOCK)) * s[None, None, :]).reshape(BS, G * BLOCK)),
            "w1": bf(np.random.standard_normal((G, BLOCK, HID)) / np.sqrt(BLOCK) / s[None, :, None]),
            "b1": bf(np.random.standard_normal((G, 1, HID)) * 0.2),
            "w2": bf(np.random.standard_normal((G, HID, BLOCK)) / np.sqrt(HID)),
            "b2": bf(np.random.standard_normal((G, 1, BLOCK)) * 0.2)}


def reference(x_blocks, w1, b1, w2, b2):
    y = f64(x_blocks)
    bs = y.shape[0]
    z = y.reshape(bs, -1, BLOCK).transpose(1, 0, 2)
    h = elu((mxq(z, 2, "e4m3") @ mxq(f64(w1), 1, "e4m3")) + f64(b1))
    h = (mxq(h, 2, "e4m3") @ mxq(f64(w2), 1, "e4m3")) + f64(b2)
    z = h + z
    return z.transpose(1, 0, 2).reshape(bs, -1)

@@ -1,0 +1,229 @@
+from contextlib import ExitStack
+
+import concourse.mybir as mybir
+from concourse.masks import make_identity
+
+F32 = mybir.dt.float32
+BF16 = mybir.dt.bfloat16
+U32 = mybir.dt.uint32
+U8 = mybir.dt.uint8
+FP8X4 = mybir.dt.float8_e4m3fn_x4
+ACT = mybir.ActivationFunctionType
+ALU = mybir.AluOpType
+
+P = 128
+PACK = 4
+ROWS = 4096
+GROUPS = 2
+FEAT = 512
+WIDTH = GROUPS * FEAT
+CHUNK = 512
+ROW_TILES = CHUNK // P
+N_CHUNKS = ROWS // CHUNK
+N_PIECES = N_CHUNKS * GROUPS
+
+FLOPS = 2 * 2 * ROWS * GROUPS * FEAT * FEAT
+
+
+def tile_blockresmlp_mixerblock_pb_t_kernel(tc, x_blocks, w1, b1, w2, b2, out):
+    nc = tc.nc
+    with ExitStack() as ctx:
+        keep = ctx.enter_context(tc.tile_pool(name="keep", bufs=1))
+        stage = ctx.enter_context(tc.tile_pool(name="stage", bufs=2))
+        x_pool = ctx.enter_context(tc.tile_pool(name="x", bufs=N_CHUNKS))
+        sum_pool = ctx.enter_context(tc.tile_pool(name="sum", bufs=3))
+        work = ctx.enter_context(tc.tile_pool(name="work", bufs=2))
+        psum_xt = ctx.enter_context(tc.psum_pool(name="psum_xt", bufs=2))
+        psum_l1 = ctx.enter_context(tc.psum_pool(name="psum_l1", bufs=3))
+        psum_l2 = ctx.enter_context(tc.psum_pool(name="psum_l2", bufs=3))
+
+        def chunk_rows(dram, c):
+            return dram[c * CHUNK : (c + 1) * CHUNK, :]
+
+        x_sb = {}
+
+        def load_x(c):
+            x_sb[c] = x_pool.tile([P, ROW_TILES * WIDTH], BF16, name="x_sb")
+            nc.sync.dma_start(
+                out=x_sb[c][:], in_=chunk_rows(x_blocks, c).rearrange("(p r) d -> p (r d)", r=ROW_TILES)
+            )
+
+        w_raw = {}
+
+        def load_w(n):
+            w_raw[1, n] = stage.tile([P, PACK, FEAT], BF16, name="w1_raw")
+            nc.sync.dma_start(
+                out=w_raw[1, n][:].rearrange("p (u e) h -> p u (e h)", e=2),
+                in_=w1[n].rearrange("(u p e) h -> p u (e h)", u=2, e=2),
+            )
+            w_raw[2, n] = stage.tile([P, PACK, FEAT], BF16, name="w2_raw")
+            nc.sync.dma_start(out=w_raw[2, n][:], in_=w2[n].rearrange("(p t) d -> p t d", t=PACK))
+
+        load_x(0)
+        load_w(0)
+        b1_bf = keep.tile([P, GROUPS, PACK], BF16)
+        nc.sync.dma_start(out=b1_bf[:], in_=b1.rearrange("g o (q s) -> q (g o) s", s=PACK))
+        load_w(1)
+        for c in range(1, N_CHUNKS):
+            load_x(c)
+        b2_all = keep.tile([P, WIDTH], BF16)
+        nc.scalar.dma_start(out=b2_all[:], in_=b2.rearrange("g o d -> (g o d)").partition_broadcast(P))
+
+        ident = keep.tile([P, P], F32)
+        make_identity(nc, ident[:])
+        b1_f32 = keep.tile([P, GROUPS, PACK], F32)
+        nc.vector.tensor_copy(out=b1_f32[:], in_=b1_bf[:])
+
+        w_codes = {}
+        w_scales = {}
+        for layer in (1, 2):
+            w_codes[layer] = keep.tile([P, GROUPS, FEAT], U32, align_bytes=64, name="w%d_codes" % layer)
+            w_scales[layer] = keep.tile([P, GROUPS, FEAT], U8, align_bytes=64, name="w%d_scales" % layer)
+
+        def quantise_w(layer, n):
+            grouped = stage.tile([P, FEAT, PACK], BF16, align_bytes=64, name="w_grouped")
+            if layer == 1:
+                nc.vector.tensor_copy(
+                    out=grouped[:].rearrange("p (s q) t -> p s q t", s=PACK),
+                    in_=w_raw[layer, n][:].rearrange("p t (q s) -> p s q t", s=PACK),
+                )
+            else:
+                nc.vector.tensor_copy(out=grouped[:], in_=w_raw[layer, n][:].rearrange("p t d -> p d t"))
+            nc.vector.quantize_mx(
+                out=w_codes[layer][:, n, :].bitcast(FP8X4),
+                scales=w_scales[layer][:, n, :],
+                in_=grouped[:].rearrange("p c t -> p (c t)"),
+            )
+
+        x_plus_b2 = {}
+        xt_banks = {}
+        grouped_x = {}
+        acc1 = {}
+        h_planes = {}
+        grouped_h = {}
+        acc2 = {}
+
+        def add_b2(c):
+            x_plus_b2[c] = sum_pool.tile([P, ROW_TILES, WIDTH], F32, name="x_plus_b2")
+            for r in range(ROW_TILES):
+                nc.gpsimd.tensor_tensor(
+                    out=x_plus_b2[c][:, r, :],
+                    in0=x_sb[c][:, r * WIDTH : (r + 1) * WIDTH],
+                    in1=b2_all[:],
+                    op=ALU.add,
+                )
+
+        def transpose_x(i):
+            c, n = divmod(i, GROUPS)
+            words = x_sb[c][:].bitcast(F32)
+            for half in range(2):
+                xt = psum_xt.tile([P, 2, 2 * P], F32, name="xt")
+                for k in range(2):
+                    for u in range(2):
+                        first = ((2 * half + k) * WIDTH + n * FEAT) // 2 + u * P
+                        nc.tensor.transpose(xt[:, u, k * P : (k + 1) * P], words[:, first : first + P], ident[:])
+                xt_banks[i, half] = xt
+
+        def regroup_x(i):
+            grouped_x[i] = work.tile([P, CHUNK * PACK], BF16, align_bytes=64, name="grouped_x")
+            pairs = grouped_x[i][:].bitcast(F32).rearrange("p (b u) -> p b u", u=2)
+            for half in range(2):
+                nc.scalar.copy(
+                    out=pairs[:, half * 2 * P : (half + 1) * 2 * P, :],
+                    in_=xt_banks[i, half][:].rearrange("p u b -> p b u"),
+                )
+
+        def layer1(i):
+            n = i % GROUPS
+            x_codes = work.tile([P, CHUNK], U32, align_bytes=64, name="x_codes")
+            x_scales = work.tile([P, CHUNK], U8, align_bytes=64, name="x_scales")
+            nc.vector.quantize_mx(out=x_codes[:].bitcast(FP8X4), scales=x_scales[:], in_=grouped_x[i][:])
+            for s in range(PACK):
+                acc1[i, s] = psum_l1.tile([P, CHUNK], F32, name="acc1")
+                nc.tensor.matmul_mx(
+                    out=acc1[i, s][:],
+                    lhsT=w_codes[1][:, n, s * P : (s + 1) * P].bitcast(FP8X4),
+                    lhsT_scale=w_scales[1][:, n, s * P : (s + 1) * P],
+                    rhs=x_codes[:].bitcast(FP8X4),
+                    rhs_scale=x_scales[:],
+                    start=True,
+                    stop=True,
+                )
+
+        def elu(i):
+            n = i % GROUPS
+            negative = work.tile([P, PACK, CHUNK], F32, name="negative")
+            h_planes[i] = work.tile([P, PACK, CHUNK], BF16, name="h_planes")
+            for s in range(PACK):
+                bias = b1_f32[:, n, s : s + 1]
+                nc.scalar.activation(out=negative[:, s, :], in_=acc1[i, s][:], func=ACT.Exp, bias=bias, scale=1.0)
+                nc.vector.tensor_scalar(
+                    out=negative[:, s, :], in0=negative[:, s, :], scalar1=-1.0, scalar2=0.0, op0=ALU.add, op1=ALU.min
+                )
+                nc.vector.scalar_tensor_tensor(
+                    out=h_planes[i][:, s, :],
+                    in0=acc1[i, s][:],
+                    scalar=bias,
+                    in1=negative[:, s, :],
+                    op0=ALU.add,
+                    op1=ALU.max,
+                )
+
+        def regroup_h(i):
+            grouped_h[i] = work.tile([P, CHUNK, PACK], BF16, align_bytes=64, name="grouped_h")
+            nc.scalar.copy(out=grouped_h[i][:], in_=h_planes[i][:].rearrange("p s b -> p b s"))
+
+        def layer2(i):
+            n = i % GROUPS
+            h_codes = work.tile([P, CHUNK], U32, align_bytes=64, name="h_codes")
+            h_scales = work.tile([P, CHUNK], U8, align_bytes=64, name="h_scales")
+            nc.vector.quantize_mx(
+                out=h_codes[:].bitcast(FP8X4), scales=h_scales[:], in_=grouped_h[i][:].rearrange("p b s -> p (b s)")
+            )
+            for r in range(ROW_TILES):
+                acc2[i, r] = psum_l2.tile([P, FEAT], F32, name="acc2")
+                nc.tensor.matmul_mx(
+                    out=acc2[i, r][:],
+                    lhsT=h_codes[:, r * P : (r + 1) * P].bitcast(FP8X4),
+                    lhsT_scale=h_scales[:, r * P : (r + 1) * P],
+                    rhs=w_codes[2][:, n, :].bitcast(FP8X4),
+                    rhs_scale=w_scales[2][:, n, :],
+                    start=True,
+                    stop=True,
+                )
+
+        def finish(i):
+            c, n = divmod(i, GROUPS)
+            cols = slice(n * FEAT, (n + 1) * FEAT)
+            for r in range(ROW_TILES):
+                total = x_plus_b2[c][:, r, cols]
+                nc.vector.tensor_tensor(out=total, in0=acc2[i, r][:], in1=total, op=ALU.add)
+            nc.sync.dma_start(
+                out=chunk_rows(out, c)[:, cols].rearrange("(p r) d -> p r d", r=ROW_TILES),
+                in_=x_plus_b2[c][:, :, cols],
+            )
+
+        quantise_w(1, 0)
+        transpose_x(0)
+        regroup_x(0)
+        layer1(0)
+        transpose_x(1)
+        quantise_w(1, 1)
+        quantise_w(2, 0)
+        quantise_w(2, 1)
+        add_b2(0)
+        for i in range(N_PIECES):
+            if i % GROUPS == 0 and i // GROUPS + 1 < N_CHUNKS:
+                add_b2(i // GROUPS + 1)
+            elu(i)
+            if i + 1 < N_PIECES:
+                regroup_x(i + 1)
+            regroup_h(i)
+            if i + 1 < N_PIECES:
+                layer1(i + 1)
+            if i + 2 < N_PIECES:
+                transpose_x(i + 2)
+            if i >= 1:
+                finish(i - 1)
+            layer2(i)
+        finish(N_PIECES - 1)

@@ -31,11 +31,9 @@ def tile_blockresmlp_mixerblock_pb_t_kernel(tc, x_blocks, w1, b1, w2, b2, out):
         keep = ctx.enter_context(tc.tile_pool(name="keep", bufs=1))
         stage = ctx.enter_context(tc.tile_pool(name="stage", bufs=2))
         x_pool = ctx.enter_context(tc.tile_pool(name="x", bufs=N_CHUNKS))
-        sum_pool = ctx.enter_context(tc.tile_pool(name="sum", bufs=3))
         work = ctx.enter_context(tc.tile_pool(name="work", bufs=2))
-        psum_xt = ctx.enter_context(tc.psum_pool(name="psum_xt", bufs=2))
-        psum_l1 = ctx.enter_context(tc.psum_pool(name="psum_l1", bufs=3))
-        psum_l2 = ctx.enter_context(tc.psum_pool(name="psum_l2", bufs=3))
+        out_pool = ctx.enter_context(tc.tile_pool(name="out", bufs=3))
+        psum = ctx.enter_context(tc.psum_pool(name="psum", bufs=2))
 
         def chunk_rows(dram, c):
             return dram[c * CHUNK : (c + 1) * CHUNK, :]
@@ -59,20 +57,23 @@ def tile_blockresmlp_mixerblock_pb_t_kernel(tc, x_blocks, w1, b1, w2, b2, out):
             w_raw[2, n] = stage.tile([P, PACK, FEAT], BF16, name="w2_raw")
             nc.sync.dma_start(out=w_raw[2, n][:], in_=w2[n].rearrange("(p t) d -> p t d", t=PACK))
 
+        def load_bias(dram, name):
+            as_given = keep.tile([P, GROUPS, PACK], BF16, name=name + "_bf16")
+            nc.sync.dma_start(out=as_given[:], in_=dram.rearrange("g o (q s) -> q (g o) s", s=PACK))
+            widened = keep.tile([P, GROUPS, PACK], F32, name=name + "_f32")
+            nc.vector.tensor_copy(out=widened[:], in_=as_given[:])
+            return widened
+
         load_x(0)
         load_w(0)
-        b1_bf = keep.tile([P, GROUPS, PACK], BF16)
-        nc.sync.dma_start(out=b1_bf[:], in_=b1.rearrange("g o (q s) -> q (g o) s", s=PACK))
+        b1_sb = load_bias(b1, "b1")
+        b2_sb = load_bias(b2, "b2")
         load_w(1)
         for c in range(1, N_CHUNKS):
             load_x(c)
-        b2_all = keep.tile([P, WIDTH], BF16)
-        nc.scalar.dma_start(out=b2_all[:], in_=b2.rearrange("g o d -> (g o d)").partition_broadcast(P))
 
         ident = keep.tile([P, P], F32)
         make_identity(nc, ident[:])
-        b1_f32 = keep.tile([P, GROUPS, PACK], F32)
-        nc.vector.tensor_copy(out=b1_f32[:], in_=b1_bf[:])
 
         w_codes = {}
         w_scales = {}
@@ -82,42 +83,47 @@ def tile_blockresmlp_mixerblock_pb_t_kernel(tc, x_blocks, w1, b1, w2, b2, out):
 
         def quantise_w(layer, n):
             grouped = stage.tile([P, FEAT, PACK], BF16, align_bytes=64, name="w_grouped")
-            if layer == 1:
-                nc.vector.tensor_copy(
-                    out=grouped[:].rearrange("p (s q) t -> p s q t", s=PACK),
-                    in_=w_raw[layer, n][:].rearrange("p t (q s) -> p s q t", s=PACK),
-                )
-            else:
-                nc.vector.tensor_copy(out=grouped[:], in_=w_raw[layer, n][:].rearrange("p t d -> p d t"))
+            nc.vector.tensor_copy(
+                out=grouped[:].rearrange("p (s q) t -> p s q t", s=PACK),
+                in_=w_raw[layer, n][:].rearrange("p t (q s) -> p s q t", s=PACK),
+            )
             nc.vector.quantize_mx(
                 out=w_codes[layer][:, n, :].bitcast(FP8X4),
                 scales=w_scales[layer][:, n, :],
                 in_=grouped[:].rearrange("p c t -> p (c t)"),
             )
 
-        x_plus_b2 = {}
+        def products(layer, n, codes, scales, tag):
+            banks = []
+            for s in range(PACK):
+                acc = psum.tile([P, CHUNK], F32, name=tag)
+                nc.tensor.matmul_mx(
+                    out=acc[:],
+                    lhsT=w_codes[layer][:, n, s * P : (s + 1) * P].bitcast(FP8X4),
+                    lhsT_scale=w_scales[layer][:, n, s * P : (s + 1) * P],
+                    rhs=codes[:].bitcast(FP8X4),
+                    rhs_scale=scales[:],
+                    start=True,
+                    stop=True,
+                )
+                banks.append(acc)
+            return banks
+
         xt_banks = {}
         grouped_x = {}
         acc1 = {}
-        h_planes = {}
+        exp_v = {}
+        relu_v = {}
         grouped_h = {}
         acc2 = {}
-
-        def add_b2(c):
-            x_plus_b2[c] = sum_pool.tile([P, ROW_TILES, WIDTH], F32, name="x_plus_b2")
-            for r in range(ROW_TILES):
-                nc.gpsimd.tensor_tensor(
-                    out=x_plus_b2[c][:, r, :],
-                    in0=x_sb[c][:, r * WIDTH : (r + 1) * WIDTH],
-                    in1=b2_all[:],
-                    op=ALU.add,
-                )
+        result_t = {}
+        back_banks = {}
 
         def transpose_x(i):
             c, n = divmod(i, GROUPS)
             words = x_sb[c][:].bitcast(F32)
             for half in range(2):
-                xt = psum_xt.tile([P, 2, 2 * P], F32, name="xt")
+                xt = psum.tile([P, 2, 2 * P], F32, name="xt")
                 for k in range(2):
                     for u in range(2):
                         first = ((2 * half + k) * WIDTH + n * FEAT) // 2 + u * P
@@ -128,102 +134,99 @@ def tile_blockresmlp_mixerblock_pb_t_kernel(tc, x_blocks, w1, b1, w2, b2, out):
             grouped_x[i] = work.tile([P, CHUNK * PACK], BF16, align_bytes=64, name="grouped_x")
             pairs = grouped_x[i][:].bitcast(F32).rearrange("p (b u) -> p b u", u=2)
             for half in range(2):
-                nc.scalar.copy(
+                nc.vector.tensor_copy(
                     out=pairs[:, half * 2 * P : (half + 1) * 2 * P, :],
                     in_=xt_banks[i, half][:].rearrange("p u b -> p b u"),
                 )
 
         def layer1(i):
-            n = i % GROUPS
             x_codes = work.tile([P, CHUNK], U32, align_bytes=64, name="x_codes")
             x_scales = work.tile([P, CHUNK], U8, align_bytes=64, name="x_scales")
             nc.vector.quantize_mx(out=x_codes[:].bitcast(FP8X4), scales=x_scales[:], in_=grouped_x[i][:])
+            acc1[i] = products(1, i % GROUPS, x_codes, x_scales, "acc1")
+
+        def exp_and_relu(i):
+            n = i % GROUPS
+            exp_v[i] = work.tile([P, PACK, CHUNK], F32, name="exp_v")
+            relu_v[i] = work.tile([P, PACK, CHUNK], BF16, name="relu_v")
             for s in range(PACK):
-                acc1[i, s] = psum_l1.tile([P, CHUNK], F32, name="acc1")
-                nc.tensor.matmul_mx(
-                    out=acc1[i, s][:],
-                    lhsT=w_codes[1][:, n, s * P : (s + 1) * P].bitcast(FP8X4),
-                    lhsT_scale=w_scales[1][:, n, s * P : (s + 1) * P],
-                    rhs=x_codes[:].bitcast(FP8X4),
-                    rhs_scale=x_scales[:],
-                    start=True,
-                    stop=True,
-                )
+                bias = b1_sb[:, n, s : s + 1]
+                nc.scalar.activation(out=exp_v[i][:, s, :], in_=acc1[i][s][:], func=ACT.Exp, bias=bias, scale=1.0)
+                nc.scalar.activation(out=relu_v[i][:, s, :], in_=acc1[i][s][:], func=ACT.Relu, bias=bias, scale=1.0)
 
         def elu(i):
-            n = i % GROUPS
-            negative = work.tile([P, PACK, CHUNK], F32, name="negative")
-            h_planes[i] = work.tile([P, PACK, CHUNK], BF16, name="h_planes")
-            for s in range(PACK):
-                bias = b1_f32[:, n, s : s + 1]
-                nc.scalar.activation(out=negative[:, s, :], in_=acc1[i, s][:], func=ACT.Exp, bias=bias, scale=1.0)
-                nc.vector.tensor_scalar(
-                    out=negative[:, s, :], in0=negative[:, s, :], scalar1=-1.0, scalar2=0.0, op0=ALU.add, op1=ALU.min
-                )
-                nc.vector.scalar_tensor_tensor(
-                    out=h_planes[i][:, s, :],
-                    in0=acc1[i, s][:],
-                    scalar=bias,
-                    in1=negative[:, s, :],
-                    op0=ALU.add,
-                    op1=ALU.max,
-                )
-
-        def regroup_h(i):
             grouped_h[i] = work.tile([P, CHUNK, PACK], BF16, align_bytes=64, name="grouped_h")
-            nc.scalar.copy(out=grouped_h[i][:], in_=h_planes[i][:].rearrange("p s b -> p b s"))
+            nc.vector.scalar_tensor_tensor(
+                out=grouped_h[i][:],
+                in0=exp_v[i][:].rearrange("p s b -> p b s"),
+                scalar=1.0,
+                in1=relu_v[i][:].rearrange("p s b -> p b s"),
+                op0=ALU.subtract,
+                op1=ALU.min,
+            )
 
         def layer2(i):
-            n = i % GROUPS
             h_codes = work.tile([P, CHUNK], U32, align_bytes=64, name="h_codes")
             h_scales = work.tile([P, CHUNK], U8, align_bytes=64, name="h_scales")
             nc.vector.quantize_mx(
                 out=h_codes[:].bitcast(FP8X4), scales=h_scales[:], in_=grouped_h[i][:].rearrange("p b s -> p (b s)")
             )
-            for r in range(ROW_TILES):
-                acc2[i, r] = psum_l2.tile([P, FEAT], F32, name="acc2")
-                nc.tensor.matmul_mx(
-                    out=acc2[i, r][:],
-                    lhsT=h_codes[:, r * P : (r + 1) * P].bitcast(FP8X4),
-                    lhsT_scale=h_scales[:, r * P : (r + 1) * P],
-                    rhs=w_codes[2][:, n, :].bitcast(FP8X4),
-                    rhs_scale=w_scales[2][:, n, :],
-                    start=True,
-                    stop=True,
+            acc2[i] = products(2, i % GROUPS, h_codes, h_scales, "acc2")
+
+        def add_b2(i):
+            n = i % GROUPS
+            result_t[i] = work.tile([P, PACK, CHUNK], F32, name="result_t")
+            for s in range(PACK):
+                nc.scalar.activation(
+                    out=result_t[i][:, s, :], in_=acc2[i][s][:], func=ACT.Identity, bias=b2_sb[:, n, s : s + 1], scale=1.0
                 )
+
+        def transpose_back(i):
+            for r in range(ROW_TILES):
+                back = psum.tile([P, PACK, P], F32, name="back")
+                for s in range(PACK):
+                    nc.tensor.transpose(back[:, s, :], result_t[i][:, s, r * P : (r + 1) * P], ident[:])
+                back_banks[i, r] = back
 
         def finish(i):
             c, n = divmod(i, GROUPS)
-            cols = slice(n * FEAT, (n + 1) * FEAT)
+            out_sb = out_pool.tile([P, ROW_TILES, FEAT], F32, name="out_sb")
             for r in range(ROW_TILES):
-                total = x_plus_b2[c][:, r, cols]
-                nc.vector.tensor_tensor(out=total, in0=acc2[i, r][:], in1=total, op=ALU.add)
+                first = r * WIDTH + n * FEAT
+                nc.vector.tensor_tensor(
+                    out=out_sb[:, r, :].rearrange("b (q s) -> b q s", s=PACK),
+                    in0=back_banks[i, r][:].rearrange("b s q -> b q s"),
+                    in1=x_sb[c][:, first : first + FEAT].rearrange("b (q s) -> b q s", s=PACK),
+                    op=ALU.add,
+                )
             nc.sync.dma_start(
-                out=chunk_rows(out, c)[:, cols].rearrange("(p r) d -> p r d", r=ROW_TILES),
-                in_=x_plus_b2[c][:, :, cols],
+                out=chunk_rows(out, c)[:, n * FEAT : (n + 1) * FEAT].rearrange("(p r) d -> p r d", r=ROW_TILES),
+                in_=out_sb[:],
             )
 
         quantise_w(1, 0)
         transpose_x(0)
         regroup_x(0)
         layer1(0)
-        transpose_x(1)
         quantise_w(1, 1)
         quantise_w(2, 0)
         quantise_w(2, 1)
-        add_b2(0)
-        for i in range(N_PIECES):
-            if i % GROUPS == 0 and i // GROUPS + 1 < N_CHUNKS:
-                add_b2(i // GROUPS + 1)
-            elu(i)
+        for i in range(N_PIECES + 2):
+            if i < N_PIECES:
+                exp_and_relu(i)
+            if i + 1 < N_PIECES:
+                transpose_x(i + 1)
+            if 0 <= i - 2:
+                transpose_back(i - 2)
+            if 0 <= i - 1 < N_PIECES:
+                elu(i - 1)
             if i + 1 < N_PIECES:
                 regroup_x(i + 1)
-            regroup_h(i)
+            if 0 <= i - 1 < N_PIECES:
+                layer2(i - 1)
             if i + 1 < N_PIECES:
                 layer1(i + 1)
-            if i + 2 < N_PIECES:
-                transpose_x(i + 2)
-            if i >= 1:
-                finish(i - 1)
-            layer2(i)
-        finish(N_PIECES - 1)
+            if 0 <= i - 2:
+                finish(i - 2)
+            if 0 <= i - 1 < N_PIECES:
+                add_b2(i - 1)

@@ -32,201 +32,281 @@ def tile_blockresmlp_mixerblock_pb_t_kernel(tc, x_blocks, w1, b1, w2, b2, out):
         stage = ctx.enter_context(tc.tile_pool(name="stage", bufs=2))
         x_pool = ctx.enter_context(tc.tile_pool(name="x", bufs=N_CHUNKS))
         work = ctx.enter_context(tc.tile_pool(name="work", bufs=2))
+        work3 = ctx.enter_context(tc.tile_pool(name="work3", bufs=3))
         out_pool = ctx.enter_context(tc.tile_pool(name="out", bufs=3))
-        psum = ctx.enter_context(tc.psum_pool(name="psum", bufs=2))
+        psum1 = ctx.enter_context(tc.psum_pool(name="psum1", bufs=1))
+        psum2 = ctx.enter_context(tc.psum_pool(name="psum2", bufs=2))
+        psum3 = ctx.enter_context(tc.psum_pool(name="psum3", bufs=3))
 
         def chunk_rows(dram, c):
             return dram[c * CHUNK : (c + 1) * CHUNK, :]
 
         x_sb = {}
 
-        def load_x(c):
-            x_sb[c] = x_pool.tile([P, ROW_TILES * WIDTH], BF16, name="x_sb")
+        def load_x(c, first=0, last=WIDTH):
+            if c not in x_sb:
+                x_sb[c] = x_pool.tile([P, ROW_TILES, WIDTH], BF16, name="x_sb")
             nc.sync.dma_start(
-                out=x_sb[c][:], in_=chunk_rows(x_blocks, c).rearrange("(p r) d -> p (r d)", r=ROW_TILES)
+                out=x_sb[c][:, :, first:last],
+                in_=chunk_rows(x_blocks, c)[:, first:last].rearrange("(p r) d -> p r d", r=ROW_TILES),
             )
 
         w_raw = {}
 
-        def load_w(n):
+        def load_w1(n):
             w_raw[1, n] = stage.tile([P, PACK, FEAT], BF16, name="w1_raw")
             nc.sync.dma_start(
                 out=w_raw[1, n][:].rearrange("p (u e) h -> p u (e h)", e=2),
                 in_=w1[n].rearrange("(u p e) h -> p u (e h)", u=2, e=2),
             )
+
+        def load_w2(n):
             w_raw[2, n] = stage.tile([P, PACK, FEAT], BF16, name="w2_raw")
             nc.sync.dma_start(out=w_raw[2, n][:], in_=w2[n].rearrange("(p t) d -> p t d", t=PACK))
 
         def load_bias(dram, name):
             as_given = keep.tile([P, GROUPS, PACK], BF16, name=name + "_bf16")
-            nc.sync.dma_start(out=as_given[:], in_=dram.rearrange("g o (q s) -> q (g o) s", s=PACK))
-            widened = keep.tile([P, GROUPS, PACK], F32, name=name + "_f32")
-            nc.vector.tensor_copy(out=widened[:], in_=as_given[:])
-            return widened
+            nc.scalar.dma_start(out=as_given[:], in_=dram.rearrange("g o (q s) -> q (g o) s", s=PACK))
+            return as_given
 
-        load_x(0)
-        load_w(0)
-        b1_sb = load_bias(b1, "b1")
-        b2_sb = load_bias(b2, "b2")
-        load_w(1)
-        for c in range(1, N_CHUNKS):
+        load_x(0, 0, FEAT)
+        load_w1(0)
+        b1_bf = load_bias(b1, "b1")
+        b2_bf = load_bias(b2, "b2")
+        load_x(0, FEAT, WIDTH)
+        load_w1(1)
+        load_w2(0)
+        load_x(1)
+        load_w2(1)
+        for c in range(2, N_CHUNKS):
             load_x(c)
 
         ident = keep.tile([P, P], F32)
         make_identity(nc, ident[:])
+        b1_sb = keep.tile([P, GROUPS, PACK], F32)
+        b1_plus_1 = keep.tile([P, GROUPS, PACK], F32)
+        b2_sb = keep.tile([P, GROUPS, PACK], F32)
 
         w_codes = {}
         w_scales = {}
+        w_grouped = {}
         for layer in (1, 2):
-            w_codes[layer] = keep.tile([P, GROUPS, FEAT], U32, align_bytes=64, name="w%d_codes" % layer)
-            w_scales[layer] = keep.tile([P, GROUPS, FEAT], U8, align_bytes=64, name="w%d_scales" % layer)
+            for n in range(GROUPS):
+                w_codes[layer, n] = keep.tile([P, FEAT], U32, align_bytes=64, name="w%d_%d_codes" % (layer, n))
+                w_scales[layer, n] = keep.tile([P, FEAT], U8, align_bytes=64, name="w%d_%d_scales" % (layer, n))
+
+        def regroup_w(layer, n, engine):
+            w_grouped[layer, n] = stage.tile([P, FEAT, PACK], BF16, align_bytes=64, name="w_grouped")
+            dst = w_grouped[layer, n][:].rearrange("p (s q) t -> p s q t", s=PACK)
+            src = w_raw[layer, n][:].rearrange("p t (q s) -> p s q t", s=PACK)
+            if engine is nc.gpsimd:
+                for s in range(PACK):
+                    nc.gpsimd.tensor_scalar(
+                        out=dst[:, s], in0=src[:, s], scalar1=1.0, scalar2=0.0, op0=ALU.mult, op1=ALU.add
+                    )
+            else:
+                nc.vector.tensor_copy(out=dst, in_=src)
 
         def quantise_w(layer, n):
-            grouped = stage.tile([P, FEAT, PACK], BF16, align_bytes=64, name="w_grouped")
-            nc.vector.tensor_copy(
-                out=grouped[:].rearrange("p (s q) t -> p s q t", s=PACK),
-                in_=w_raw[layer, n][:].rearrange("p t (q s) -> p s q t", s=PACK),
-            )
             nc.vector.quantize_mx(
-                out=w_codes[layer][:, n, :].bitcast(FP8X4),
-                scales=w_scales[layer][:, n, :],
-                in_=grouped[:].rearrange("p c t -> p (c t)"),
+                out=w_codes[layer, n][:].bitcast(FP8X4),
+                scales=w_scales[layer, n][:],
+                in_=w_grouped[layer, n][:].rearrange("p c t -> p (c t)"),
             )
 
-        def products(layer, n, codes, scales, tag):
-            banks = []
-            for s in range(PACK):
-                acc = psum.tile([P, CHUNK], F32, name=tag)
-                nc.tensor.matmul_mx(
-                    out=acc[:],
-                    lhsT=w_codes[layer][:, n, s * P : (s + 1) * P].bitcast(FP8X4),
-                    lhsT_scale=w_scales[layer][:, n, s * P : (s + 1) * P],
-                    rhs=codes[:].bitcast(FP8X4),
-                    rhs_scale=scales[:],
-                    start=True,
-                    stop=True,
-                )
-                banks.append(acc)
-            return banks
-
-        xt_banks = {}
+        xt = {}
         grouped_x = {}
+        x_q = {}
         acc1 = {}
         exp_v = {}
-        relu_v = {}
+        elu_1 = {}
         grouped_h = {}
+        h_q = {}
         acc2 = {}
         result_t = {}
-        back_banks = {}
+        back = {}
+        out_sb = {}
 
-        def transpose_x(i):
+        def transpose_x(i, half):
             c, n = divmod(i, GROUPS)
             words = x_sb[c][:].bitcast(F32)
-            for half in range(2):
-                xt = psum.tile([P, 2, 2 * P], F32, name="xt")
-                for k in range(2):
-                    for u in range(2):
-                        first = ((2 * half + k) * WIDTH + n * FEAT) // 2 + u * P
-                        nc.tensor.transpose(xt[:, u, k * P : (k + 1) * P], words[:, first : first + P], ident[:])
-                xt_banks[i, half] = xt
+            bank = psum1.tile([P, 2, 2 * P], F32, name="xt")
+            for k in range(2):
+                for u in range(2):
+                    first = n * FEAT // 2 + u * P
+                    nc.tensor.transpose(
+                        bank[:, u, k * P : (k + 1) * P], words[:, 2 * half + k, first : first + P], ident[:]
+                    )
+            xt[i, half] = bank
 
-        def regroup_x(i):
-            grouped_x[i] = work.tile([P, CHUNK * PACK], BF16, align_bytes=64, name="grouped_x")
+        def regroup_x(i, half):
+            if half == 0:
+                grouped_x[i] = work.tile([P, CHUNK * PACK], BF16, align_bytes=64, name="grouped_x")
             pairs = grouped_x[i][:].bitcast(F32).rearrange("p (b u) -> p b u", u=2)
-            for half in range(2):
-                nc.vector.tensor_copy(
-                    out=pairs[:, half * 2 * P : (half + 1) * 2 * P, :],
-                    in_=xt_banks[i, half][:].rearrange("p u b -> p b u"),
-                )
+            nc.scalar.copy(
+                out=pairs[:, half * 2 * P : (half + 1) * 2 * P, :], in_=xt[i, half][:].rearrange("p u b -> p b u")
+            )
 
-        def layer1(i):
-            x_codes = work.tile([P, CHUNK], U32, align_bytes=64, name="x_codes")
-            x_scales = work.tile([P, CHUNK], U8, align_bytes=64, name="x_scales")
-            nc.vector.quantize_mx(out=x_codes[:].bitcast(FP8X4), scales=x_scales[:], in_=grouped_x[i][:])
-            acc1[i] = products(1, i % GROUPS, x_codes, x_scales, "acc1")
+        def quantise_x(i):
+            codes = work.tile([P, CHUNK], U32, align_bytes=64, name="x_codes")
+            scales = work.tile([P, CHUNK], U8, align_bytes=64, name="x_scales")
+            nc.vector.quantize_mx(out=codes[:].bitcast(FP8X4), scales=scales[:], in_=grouped_x[i][:])
+            x_q[i] = (codes, scales)
 
-        def exp_and_relu(i):
+        def product(layer, i, s, operand, pool, name):
             n = i % GROUPS
-            exp_v[i] = work.tile([P, PACK, CHUNK], F32, name="exp_v")
-            relu_v[i] = work.tile([P, PACK, CHUNK], BF16, name="relu_v")
-            for s in range(PACK):
-                bias = b1_sb[:, n, s : s + 1]
-                nc.scalar.activation(out=exp_v[i][:, s, :], in_=acc1[i][s][:], func=ACT.Exp, bias=bias, scale=1.0)
-                nc.scalar.activation(out=relu_v[i][:, s, :], in_=acc1[i][s][:], func=ACT.Relu, bias=bias, scale=1.0)
+            codes, scales = operand
+            bank = pool.tile([P, CHUNK], F32, name=name)
+            nc.tensor.matmul_mx(
+                out=bank[:],
+                lhsT=w_codes[layer, n][:, s * P : (s + 1) * P].bitcast(FP8X4),
+                lhsT_scale=w_scales[layer, n][:, s * P : (s + 1) * P],
+                rhs=codes[:].bitcast(FP8X4),
+                rhs_scale=scales[:],
+                start=True,
+                stop=True,
+            )
+            return bank
 
-        def elu(i):
-            grouped_h[i] = work.tile([P, CHUNK, PACK], BF16, align_bytes=64, name="grouped_h")
+        def layer1(i, s):
+            acc1[i, s] = product(1, i, s, x_q[i], psum3, "acc1")
+
+        def exponential(i, s):
+            n = i % GROUPS
+            if s == 0:
+                exp_v[i] = work3.tile([P, PACK, CHUNK], F32, name="exp_v")
+            nc.scalar.activation(
+                out=exp_v[i][:, s, :], in_=acc1[i, s][:], func=ACT.Exp, bias=b1_sb[:, n, s : s + 1], scale=1.0
+            )
+
+        def clamp(i, s):
+            e = exp_v[i][:, s, :]
+            nc.gpsimd.tensor_scalar(out=e, in0=e, scalar1=1.0, scalar2=0.0, op0=ALU.min, op1=ALU.max)
+
+        def maximum(i, s):
+            n = i % GROUPS
+            if s == 0:
+                elu_1[i] = work.tile([P, PACK, CHUNK], F32, name="elu_1")
             nc.vector.scalar_tensor_tensor(
-                out=grouped_h[i][:],
-                in0=exp_v[i][:].rearrange("p s b -> p b s"),
-                scalar=1.0,
-                in1=relu_v[i][:].rearrange("p s b -> p b s"),
-                op0=ALU.subtract,
-                op1=ALU.min,
+                out=elu_1[i][:, s, :],
+                in0=acc1[i, s][:],
+                scalar=b1_plus_1[:, n, s : s + 1],
+                in1=exp_v[i][:, s, :],
+                op0=ALU.add,
+                op1=ALU.max,
             )
 
-        def layer2(i):
-            h_codes = work.tile([P, CHUNK], U32, align_bytes=64, name="h_codes")
-            h_scales = work.tile([P, CHUNK], U8, align_bytes=64, name="h_scales")
+        def regroup_h(i, half):
+            if half == 0:
+                grouped_h[i] = work.tile([P, CHUNK, PACK], BF16, align_bytes=64, name="grouped_h")
+            rows = slice(half * CHUNK // 2, (half + 1) * CHUNK // 2)
+            nc.vector.tensor_scalar(
+                out=grouped_h[i][:, rows, :],
+                in0=elu_1[i][:, :, rows].rearrange("p s b -> p b s"),
+                scalar1=-1.0,
+                scalar2=None,
+                op0=ALU.add,
+            )
+
+        def quantise_h(i):
+            codes = work.tile([P, CHUNK], U32, align_bytes=64, name="h_codes")
+            scales = work.tile([P, CHUNK], U8, align_bytes=64, name="h_scales")
             nc.vector.quantize_mx(
-                out=h_codes[:].bitcast(FP8X4), scales=h_scales[:], in_=grouped_h[i][:].rearrange("p b s -> p (b s)")
+                out=codes[:].bitcast(FP8X4), scales=scales[:], in_=grouped_h[i][:].rearrange("p b s -> p (b s)")
             )
-            acc2[i] = products(2, i % GROUPS, h_codes, h_scales, "acc2")
+            h_q[i] = (codes, scales)
 
-        def add_b2(i):
+        def layer2(i, s):
+            acc2[i, s] = product(2, i, s, h_q[i], psum2, "acc2")
+
+        def add_b2(i, s):
             n = i % GROUPS
-            result_t[i] = work.tile([P, PACK, CHUNK], F32, name="result_t")
-            for s in range(PACK):
-                nc.scalar.activation(
-                    out=result_t[i][:, s, :], in_=acc2[i][s][:], func=ACT.Identity, bias=b2_sb[:, n, s : s + 1], scale=1.0
-                )
-
-        def transpose_back(i):
-            for r in range(ROW_TILES):
-                back = psum.tile([P, PACK, P], F32, name="back")
-                for s in range(PACK):
-                    nc.tensor.transpose(back[:, s, :], result_t[i][:, s, r * P : (r + 1) * P], ident[:])
-                back_banks[i, r] = back
-
-        def finish(i):
-            c, n = divmod(i, GROUPS)
-            out_sb = out_pool.tile([P, ROW_TILES, FEAT], F32, name="out_sb")
-            for r in range(ROW_TILES):
-                first = r * WIDTH + n * FEAT
-                nc.vector.tensor_tensor(
-                    out=out_sb[:, r, :].rearrange("b (q s) -> b q s", s=PACK),
-                    in0=back_banks[i, r][:].rearrange("b s q -> b q s"),
-                    in1=x_sb[c][:, first : first + FEAT].rearrange("b (q s) -> b q s", s=PACK),
-                    op=ALU.add,
-                )
-            nc.sync.dma_start(
-                out=chunk_rows(out, c)[:, n * FEAT : (n + 1) * FEAT].rearrange("(p r) d -> p r d", r=ROW_TILES),
-                in_=out_sb[:],
+            if s == 0:
+                result_t[i] = work.tile([P, PACK, CHUNK], F32, name="result_t")
+            nc.scalar.activation(
+                out=result_t[i][:, s, :], in_=acc2[i, s][:], func=ACT.Identity, bias=b2_sb[:, n, s : s + 1], scale=1.0
             )
 
-        quantise_w(1, 0)
-        transpose_x(0)
-        regroup_x(0)
-        layer1(0)
-        quantise_w(1, 1)
-        quantise_w(2, 0)
-        quantise_w(2, 1)
-        for i in range(N_PIECES + 2):
-            if i < N_PIECES:
-                exp_and_relu(i)
-            if i + 1 < N_PIECES:
-                transpose_x(i + 1)
-            if 0 <= i - 2:
-                transpose_back(i - 2)
-            if 0 <= i - 1 < N_PIECES:
-                elu(i - 1)
-            if i + 1 < N_PIECES:
-                regroup_x(i + 1)
-            if 0 <= i - 1 < N_PIECES:
-                layer2(i - 1)
-            if i + 1 < N_PIECES:
-                layer1(i + 1)
-            if 0 <= i - 2:
-                finish(i - 2)
-            if 0 <= i - 1 < N_PIECES:
-                add_b2(i - 1)
+        def transpose_back(i, r):
+            bank = psum2.tile([P, PACK, P], F32, name="back")
+            for s in range(PACK):
+                nc.tensor.transpose(bank[:, s, :], result_t[i][:, s, r * P : (r + 1) * P], ident[:])
+            back[i, r] = bank
+
+        def finish(i, r):
+            c, n = divmod(i, GROUPS)
+            if r == 0:
+                out_sb[i] = out_pool.tile([P, ROW_TILES, FEAT], F32, name="out_sb")
+            nc.vector.tensor_tensor(
+                out=out_sb[i][:, r, :].rearrange("b (q s) -> b q s", s=PACK),
+                in0=back[i, r][:].rearrange("b s q -> b q s"),
+                in1=x_sb[c][:, r, n * FEAT : (n + 1) * FEAT].rearrange("b (q s) -> b q s", s=PACK),
+                op=ALU.add,
+            )
+            if r == ROW_TILES - 1:
+                nc.sync.dma_start(
+                    out=chunk_rows(out, c)[:, n * FEAT : (n + 1) * FEAT].rearrange("(p r) d -> p r d", r=ROW_TILES),
+                    in_=out_sb[i][:],
+                )
+
+        def is_piece(i):
+            return 0 <= i < N_PIECES
+
+        def slot_products(j):
+            i, s = divmod(j, PACK)
+            if is_piece(i):
+                layer1(i, s)
+            if is_piece(i - 2):
+                layer2(i - 2, s)
+
+        def slot(j):
+            i, k = divmod(j, PACK)
+            if is_piece(i - 3):
+                transpose_back(i - 3, k)
+            if k in (0, 2) and is_piece(i + 2):
+                transpose_x(i + 2, k // 2)
+            if is_piece(i):
+                exponential(i, k)
+                clamp(i, k)
+            if k in (1, 3) and is_piece(i + 2):
+                regroup_x(i + 2, k // 2)
+            if is_piece(i - 2):
+                add_b2(i - 2, k)
+            before = j - 1
+            if is_piece(before // PACK):
+                maximum(before // PACK, before % PACK)
+            if k == 0 and is_piece(i + 1):
+                quantise_x(i + 1)
+            if k in (1, 2) and is_piece(i - 1):
+                regroup_h(i - 1, k - 1)
+            if k == 3 and is_piece(i - 1):
+                quantise_h(i - 1)
+            if is_piece(i - 3):
+                finish(i - 3, k)
+            slot_products(j + 1)
+
+        with tc.manual_schedule(engines={mybir.EngineType.PE, mybir.EngineType.Activation, mybir.EngineType.DVE, mybir.EngineType.Pool}):
+            transpose_x(0, 0)
+            regroup_x(0, 0)
+            transpose_x(0, 1)
+            regroup_w(1, 0, nc.vector)
+            nc.vector.tensor_copy(out=b1_sb[:], in_=b1_bf[:])
+            quantise_w(1, 0)
+            regroup_x(0, 1)
+            nc.vector.tensor_copy(out=b2_sb[:], in_=b2_bf[:])
+            nc.vector.tensor_scalar_add(out=b1_plus_1[:], in0=b1_bf[:], scalar1=1.0)
+            quantise_x(0)
+            slot_products(0)
+            regroup_w(1, 1, nc.vector)
+            transpose_x(1, 0)
+            regroup_x(1, 0)
+            quantise_w(1, 1)
+            transpose_x(1, 1)
+            regroup_x(1, 1)
+            regroup_w(2, 0, nc.vector)
+            quantise_w(2, 0)
+            for j in range(PACK * (N_PIECES + 3)):
+                if j == PACK:
+                    regroup_w(2, 1, nc.vector)
+                    quantise_w(2, 1)
+                slot(j)

@@ -16,40 +16,56 @@ PACK = 4
 ROWS = 4096
 GROUPS = 2
 FEAT = 512
-WIDTH = GROUPS * FEAT
-CHUNK = 512
-ROW_TILES = CHUNK // P
-N_CHUNKS = ROWS // CHUNK
-N_PIECES = N_CHUNKS * GROUPS
+HALF = 256
+
+SIZES = (512,) * 8
+X_BUFS = 16
+H_SPLIT = 384
+B2_LAG = 9
+BACK_LAG = 13
 
 FLOPS = 2 * 2 * ROWS * GROUPS * FEAT * FEAT
 
 
 def tile_blockresmlp_mixerblock_pb_t_kernel(tc, x_blocks, w1, b1, w2, b2, out):
     nc = tc.nc
+    pieces = []
+    first_row = 0
+    for rows in SIZES:
+        for n in range(GROUPS):
+            pieces.append((first_row, rows, n))
+        first_row += rows
+    assert first_row == ROWS
+    n_pieces = len(pieces)
+    n_slots = PACK * n_pieces
+
     with ExitStack() as ctx:
         keep = ctx.enter_context(tc.tile_pool(name="keep", bufs=1))
         stage = ctx.enter_context(tc.tile_pool(name="stage", bufs=2))
-        x_pool = ctx.enter_context(tc.tile_pool(name="x", bufs=N_CHUNKS))
-        work = ctx.enter_context(tc.tile_pool(name="work", bufs=2))
-        work3 = ctx.enter_context(tc.tile_pool(name="work3", bufs=3))
+        x_pool = ctx.enter_context(tc.tile_pool(name="x", bufs=X_BUFS))
+        work = ctx.enter_context(tc.tile_pool(name="work", bufs=3))
+        work2 = ctx.enter_context(tc.tile_pool(name="work2", bufs=2))
         out_pool = ctx.enter_context(tc.tile_pool(name="out", bufs=3))
-        psum1 = ctx.enter_context(tc.psum_pool(name="psum1", bufs=1))
-        psum2 = ctx.enter_context(tc.psum_pool(name="psum2", bufs=2))
-        psum3 = ctx.enter_context(tc.psum_pool(name="psum3", bufs=3))
+        psum_xt = ctx.enter_context(tc.psum_pool(name="psum_xt", bufs=1))
+        psum_acc1 = ctx.enter_context(tc.psum_pool(name="psum_acc1", bufs=3))
+        psum_acc2 = ctx.enter_context(tc.psum_pool(name="psum_acc2", bufs=2))
+        psum_back = ctx.enter_context(tc.psum_pool(name="psum_back", bufs=2))
 
-        def chunk_rows(dram, c):
-            return dram[c * CHUNK : (c + 1) * CHUNK, :]
+        def piece_rows(dram, i):
+            r0, rows, n = pieces[i]
+            return dram[r0 : r0 + rows, n * FEAT : (n + 1) * FEAT].rearrange("(p r) d -> p r d", p=P)
+
+        def n_rows(i):
+            return pieces[i][1]
+
+        def group(i):
+            return pieces[i][2]
 
         x_sb = {}
 
-        def load_x(c, first=0, last=WIDTH):
-            if c not in x_sb:
-                x_sb[c] = x_pool.tile([P, ROW_TILES, WIDTH], BF16, name="x_sb")
-            nc.sync.dma_start(
-                out=x_sb[c][:, :, first:last],
-                in_=chunk_rows(x_blocks, c)[:, first:last].rearrange("(p r) d -> p r d", r=ROW_TILES),
-            )
+        def load_x(i):
+            x_sb[i] = x_pool.tile([P, n_rows(i) // P, FEAT], BF16, name="x_sb")
+            nc.sync.dma_start(out=x_sb[i][:], in_=piece_rows(x_blocks, i))
 
         w_raw = {}
 
@@ -69,23 +85,21 @@ def tile_blockresmlp_mixerblock_pb_t_kernel(tc, x_blocks, w1, b1, w2, b2, out):
             nc.scalar.dma_start(out=as_given[:], in_=dram.rearrange("g o (q s) -> q (g o) s", s=PACK))
             return as_given
 
-        load_x(0, 0, FEAT)
+        load_x(0)
         load_w1(0)
-        b1_bf = load_bias(b1, "b1")
-        b2_bf = load_bias(b2, "b2")
-        load_x(0, FEAT, WIDTH)
+        b1_sb = load_bias(b1, "b1")
+        b2_sb = load_bias(b2, "b2")
+        load_x(1)
         load_w1(1)
         load_w2(0)
-        load_x(1)
+        load_x(2)
         load_w2(1)
-        for c in range(2, N_CHUNKS):
-            load_x(c)
+        for i in range(3, n_pieces):
+            load_x(i)
 
         ident = keep.tile([P, P], F32)
         make_identity(nc, ident[:])
-        b1_sb = keep.tile([P, GROUPS, PACK], F32)
         b1_plus_1 = keep.tile([P, GROUPS, PACK], F32)
-        b2_sb = keep.tile([P, GROUPS, PACK], F32)
 
         w_codes = {}
         w_scales = {}
@@ -95,23 +109,20 @@ def tile_blockresmlp_mixerblock_pb_t_kernel(tc, x_blocks, w1, b1, w2, b2, out):
                 w_codes[layer, n] = keep.tile([P, FEAT], U32, align_bytes=64, name="w%d_%d_codes" % (layer, n))
                 w_scales[layer, n] = keep.tile([P, FEAT], U8, align_bytes=64, name="w%d_%d_scales" % (layer, n))
 
-        def regroup_w(layer, n, engine):
-            w_grouped[layer, n] = stage.tile([P, FEAT, PACK], BF16, align_bytes=64, name="w_grouped")
-            dst = w_grouped[layer, n][:].rearrange("p (s q) t -> p s q t", s=PACK)
-            src = w_raw[layer, n][:].rearrange("p t (q s) -> p s q t", s=PACK)
-            if engine is nc.gpsimd:
-                for s in range(PACK):
-                    nc.gpsimd.tensor_scalar(
-                        out=dst[:, s], in0=src[:, s], scalar1=1.0, scalar2=0.0, op0=ALU.mult, op1=ALU.add
-                    )
-            else:
-                nc.vector.tensor_copy(out=dst, in_=src)
+        def regroup_w(layer, n, first, last, copy):
+            if (layer, n) not in w_grouped:
+                w_grouped[layer, n] = stage.tile([P, PACK, P, PACK], BF16, align_bytes=64, name="w_grouped")
+            copy(
+                out=w_grouped[layer, n][:, first:last],
+                in_=w_raw[layer, n][:].rearrange("p t (q s) -> p s q t", s=PACK)[:, first:last],
+            )
 
-        def quantise_w(layer, n):
+        def quantise_w(layer, n, first, last):
+            cols = slice(first * P, last * P)
             nc.vector.quantize_mx(
-                out=w_codes[layer, n][:].bitcast(FP8X4),
-                scales=w_scales[layer, n][:],
-                in_=w_grouped[layer, n][:].rearrange("p c t -> p (c t)"),
+                out=w_codes[layer, n][:, cols].bitcast(FP8X4),
+                scales=w_scales[layer, n][:, cols],
+                in_=w_grouped[layer, n][:, first:last].rearrange("p s q t -> p (s q t)"),
             )
 
         xt = {}
@@ -128,35 +139,31 @@ def tile_blockresmlp_mixerblock_pb_t_kernel(tc, x_blocks, w1, b1, w2, b2, out):
         out_sb = {}
 
         def transpose_x(i, half):
-            c, n = divmod(i, GROUPS)
-            words = x_sb[c][:].bitcast(F32)
-            bank = psum1.tile([P, 2, 2 * P], F32, name="xt")
+            words = x_sb[i][:].bitcast(F32)
+            bank = psum_xt.tile([P, 2, HALF], F32, name="xt")
             for k in range(2):
                 for u in range(2):
-                    first = n * FEAT // 2 + u * P
                     nc.tensor.transpose(
-                        bank[:, u, k * P : (k + 1) * P], words[:, 2 * half + k, first : first + P], ident[:]
+                        bank[:, u, k * P : (k + 1) * P], words[:, 2 * half + k, u * P : (u + 1) * P], ident[:]
                     )
             xt[i, half] = bank
 
-        def regroup_x(i, half):
+        def regroup_x(i, half, copy):
             if half == 0:
-                grouped_x[i] = work.tile([P, CHUNK * PACK], BF16, align_bytes=64, name="grouped_x")
+                grouped_x[i] = work.tile([P, n_rows(i) * PACK], BF16, align_bytes=64, name="grouped_x")
             pairs = grouped_x[i][:].bitcast(F32).rearrange("p (b u) -> p b u", u=2)
-            nc.scalar.copy(
-                out=pairs[:, half * 2 * P : (half + 1) * 2 * P, :], in_=xt[i, half][:].rearrange("p u b -> p b u")
-            )
+            copy(out=pairs[:, half * HALF : (half + 1) * HALF, :], in_=xt[i, half][:].rearrange("p u b -> p b u"))
 
         def quantise_x(i):
-            codes = work.tile([P, CHUNK], U32, align_bytes=64, name="x_codes")
-            scales = work.tile([P, CHUNK], U8, align_bytes=64, name="x_scales")
+            codes = work.tile([P, n_rows(i)], U32, align_bytes=64, name="x_codes")
+            scales = work.tile([P, n_rows(i)], U8, align_bytes=64, name="x_scales")
             nc.vector.quantize_mx(out=codes[:].bitcast(FP8X4), scales=scales[:], in_=grouped_x[i][:])
             x_q[i] = (codes, scales)
 
         def product(layer, i, s, operand, pool, name):
-            n = i % GROUPS
+            n = group(i)
             codes, scales = operand
-            bank = pool.tile([P, CHUNK], F32, name=name)
+            bank = pool.tile([P, n_rows(i)], F32, name=name)
             nc.tensor.matmul_mx(
                 out=bank[:],
                 lhsT=w_codes[layer, n][:, s * P : (s + 1) * P].bitcast(FP8X4),
@@ -169,144 +176,143 @@ def tile_blockresmlp_mixerblock_pb_t_kernel(tc, x_blocks, w1, b1, w2, b2, out):
             return bank
 
         def layer1(i, s):
-            acc1[i, s] = product(1, i, s, x_q[i], psum3, "acc1")
+            acc1[i, s] = product(1, i, s, x_q[i], psum_acc1, "acc1")
 
         def exponential(i, s):
-            n = i % GROUPS
             if s == 0:
-                exp_v[i] = work3.tile([P, PACK, CHUNK], F32, name="exp_v")
-            nc.scalar.activation(
-                out=exp_v[i][:, s, :], in_=acc1[i, s][:], func=ACT.Exp, bias=b1_sb[:, n, s : s + 1], scale=1.0
-            )
+                exp_v[i] = work.tile([P, PACK, n_rows(i)], F32, name="exp_v")
+            bias = b1_sb[:, group(i), s : s + 1]
+            nc.scalar.activation(out=exp_v[i][:, s, :], in_=acc1[i, s][:], func=ACT.Exp, bias=bias, scale=1.0)
 
         def clamp(i, s):
             e = exp_v[i][:, s, :]
             nc.gpsimd.tensor_scalar(out=e, in0=e, scalar1=1.0, scalar2=0.0, op0=ALU.min, op1=ALU.max)
 
         def maximum(i, s):
-            n = i % GROUPS
             if s == 0:
-                elu_1[i] = work.tile([P, PACK, CHUNK], F32, name="elu_1")
+                elu_1[i] = work2.tile([P, PACK, n_rows(i)], F32, name="elu_1")
             nc.vector.scalar_tensor_tensor(
                 out=elu_1[i][:, s, :],
                 in0=acc1[i, s][:],
-                scalar=b1_plus_1[:, n, s : s + 1],
+                scalar=b1_plus_1[:, group(i), s : s + 1],
                 in1=exp_v[i][:, s, :],
                 op0=ALU.add,
                 op1=ALU.max,
             )
 
-        def regroup_h(i, half):
-            if half == 0:
-                grouped_h[i] = work.tile([P, CHUNK, PACK], BF16, align_bytes=64, name="grouped_h")
-            rows = slice(half * CHUNK // 2, (half + 1) * CHUNK // 2)
-            nc.vector.tensor_scalar(
-                out=grouped_h[i][:, rows, :],
-                in0=elu_1[i][:, :, rows].rearrange("p s b -> p b s"),
-                scalar1=-1.0,
-                scalar2=None,
-                op0=ALU.add,
-            )
+        def regroup_h(i, on_scalar):
+            if i not in grouped_h:
+                grouped_h[i] = work2.tile([P, n_rows(i), PACK], BF16, align_bytes=64, name="grouped_h")
+            rows = slice(H_SPLIT, n_rows(i)) if on_scalar else slice(0, H_SPLIT)
+            dst = grouped_h[i][:, rows, :].rearrange("p (c i) s -> p c s i", i=4)
+            src = elu_1[i][:, :, rows].rearrange("p s (c i) -> p c s i", i=4)
+            if on_scalar:
+                nc.scalar.activation(out=dst, in_=src, func=ACT.Copy, bias=-1.0, scale=1.0)
+            else:
+                nc.vector.tensor_scalar(out=dst, in0=src, scalar1=-1.0, scalar2=None, op0=ALU.add)
 
         def quantise_h(i):
-            codes = work.tile([P, CHUNK], U32, align_bytes=64, name="h_codes")
-            scales = work.tile([P, CHUNK], U8, align_bytes=64, name="h_scales")
+            codes = work.tile([P, n_rows(i)], U32, align_bytes=64, name="h_codes")
+            scales = work.tile([P, n_rows(i)], U8, align_bytes=64, name="h_scales")
             nc.vector.quantize_mx(
                 out=codes[:].bitcast(FP8X4), scales=scales[:], in_=grouped_h[i][:].rearrange("p b s -> p (b s)")
             )
             h_q[i] = (codes, scales)
 
         def layer2(i, s):
-            acc2[i, s] = product(2, i, s, h_q[i], psum2, "acc2")
+            acc2[i, s] = product(2, i, s, h_q[i], psum_acc2, "acc2")
 
         def add_b2(i, s):
-            n = i % GROUPS
             if s == 0:
-                result_t[i] = work.tile([P, PACK, CHUNK], F32, name="result_t")
-            nc.scalar.activation(
-                out=result_t[i][:, s, :], in_=acc2[i, s][:], func=ACT.Identity, bias=b2_sb[:, n, s : s + 1], scale=1.0
-            )
+                result_t[i] = work.tile([P, PACK, n_rows(i)], F32, name="result_t")
+            bias = b2_sb[:, group(i), s : s + 1]
+            nc.scalar.activation(out=result_t[i][:, s, :], in_=acc2[i, s][:], func=ACT.Identity, bias=bias, scale=1.0)
 
         def transpose_back(i, r):
-            bank = psum2.tile([P, PACK, P], F32, name="back")
+            bank = psum_back.tile([P, PACK, P], F32, name="back")
             for s in range(PACK):
                 nc.tensor.transpose(bank[:, s, :], result_t[i][:, s, r * P : (r + 1) * P], ident[:])
             back[i, r] = bank
 
         def finish(i, r):
-            c, n = divmod(i, GROUPS)
             if r == 0:
-                out_sb[i] = out_pool.tile([P, ROW_TILES, FEAT], F32, name="out_sb")
+                out_sb[i] = out_pool.tile([P, n_rows(i) // P, FEAT], F32, name="out_sb")
             nc.vector.tensor_tensor(
                 out=out_sb[i][:, r, :].rearrange("b (q s) -> b q s", s=PACK),
                 in0=back[i, r][:].rearrange("b s q -> b q s"),
-                in1=x_sb[c][:, r, n * FEAT : (n + 1) * FEAT].rearrange("b (q s) -> b q s", s=PACK),
+                in1=x_sb[i][:, r, :].rearrange("b (q s) -> b q s", s=PACK),
                 op=ALU.add,
             )
-            if r == ROW_TILES - 1:
-                nc.sync.dma_start(
-                    out=chunk_rows(out, c)[:, n * FEAT : (n + 1) * FEAT].rearrange("(p r) d -> p r d", r=ROW_TILES),
-                    in_=out_sb[i][:],
-                )
+            if r == n_rows(i) // P - 1:
+                nc.sync.dma_start(out=piece_rows(out, i), in_=out_sb[i][:])
 
         def is_piece(i):
-            return 0 <= i < N_PIECES
+            return 0 <= i < n_pieces
 
-        def slot_products(j):
-            i, s = divmod(j, PACK)
-            if is_piece(i):
-                layer1(i, s)
-            if is_piece(i - 2):
-                layer2(i - 2, s)
+        def halves(i):
+            return n_rows(i) // HALF if is_piece(i) else 0
+
+        def tiles(i):
+            return n_rows(i) // P if is_piece(i) else 0
 
         def slot(j):
             i, k = divmod(j, PACK)
-            if is_piece(i - 3):
-                transpose_back(i - 3, k)
-            if k in (0, 2) and is_piece(i + 2):
-                transpose_x(i + 2, k // 2)
             if is_piece(i):
                 exponential(i, k)
-                clamp(i, k)
-            if k in (1, 3) and is_piece(i + 2):
-                regroup_x(i + 2, k // 2)
-            if is_piece(i - 2):
-                add_b2(i - 2, k)
-            before = j - 1
-            if is_piece(before // PACK):
-                maximum(before // PACK, before % PACK)
-            if k == 0 and is_piece(i + 1):
-                quantise_x(i + 1)
-            if k in (1, 2) and is_piece(i - 1):
-                regroup_h(i - 1, k - 1)
+            if k % 2 == 1 and is_piece(i + 2):
+                regroup_x(i + 2, k // 2, nc.scalar.copy)
+            if 0 <= j - 1 < n_slots:
+                maximum(*divmod(j - 1, PACK))
+            if 0 <= j - BACK_LAG < n_slots:
+                transpose_back(*divmod(j - BACK_LAG, PACK))
             if k == 3 and is_piece(i - 1):
                 quantise_h(i - 1)
-            if is_piece(i - 3):
-                finish(i - 3, k)
-            slot_products(j + 1)
+            if 0 <= j - B2_LAG < n_slots:
+                add_b2(*divmod(j - B2_LAG, PACK))
+            if is_piece(i):
+                clamp(i, k)
+            if k % 2 == 0 and is_piece(i + 2):
+                transpose_x(i + 2, k // 2)
+            if is_piece((j + 1) // PACK):
+                layer1(*divmod(j + 1, PACK))
+            if k == 0 and is_piece(i + 1) and i >= 1:
+                quantise_x(i + 1)
+            if k == 1 and is_piece(i - 1):
+                regroup_h(i - 1, False)
+            if 0 <= j + 1 - B2_LAG < n_slots:
+                layer2(*divmod(j + 1 - B2_LAG, PACK))
+            if 0 <= j - BACK_LAG < n_slots:
+                finish(*divmod(j - BACK_LAG, PACK))
+            if k == 1 and is_piece(i - 1):
+                regroup_h(i - 1, True)
 
         with tc.manual_schedule(engines={mybir.EngineType.PE, mybir.EngineType.Activation, mybir.EngineType.DVE, mybir.EngineType.Pool}):
-            transpose_x(0, 0)
-            regroup_x(0, 0)
-            transpose_x(0, 1)
-            regroup_w(1, 0, nc.vector)
-            nc.vector.tensor_copy(out=b1_sb[:], in_=b1_bf[:])
-            quantise_w(1, 0)
-            regroup_x(0, 1)
-            nc.vector.tensor_copy(out=b2_sb[:], in_=b2_bf[:])
-            nc.vector.tensor_scalar_add(out=b1_plus_1[:], in0=b1_bf[:], scalar1=1.0)
-            quantise_x(0)
-            slot_products(0)
-            regroup_w(1, 1, nc.vector)
-            transpose_x(1, 0)
-            regroup_x(1, 0)
-            quantise_w(1, 1)
-            transpose_x(1, 1)
-            regroup_x(1, 1)
-            regroup_w(2, 0, nc.vector)
-            quantise_w(2, 0)
-            for j in range(PACK * (N_PIECES + 3)):
-                if j == PACK:
-                    regroup_w(2, 1, nc.vector)
-                    quantise_w(2, 1)
+            v_copy, s_copy = nc.vector.tensor_copy, nc.scalar.copy
+            for i in range(2):
+                for half in range(halves(i)):
+                    transpose_x(i, half)
+                    regroup_x(i, half, s_copy)
+                if i == 0:
+                    regroup_w(1, 0, 0, 1, v_copy)
+                    regroup_w(1, 0, 1, 2, v_copy)
+                    quantise_w(1, 0, 0, 2)
+                    quantise_x(0)
+            layer1(0, 0)
+            regroup_w(1, 0, 2, 4, v_copy)
+            nc.vector.tensor_scalar_add(out=b1_plus_1[:], in0=b1_sb[:], scalar1=1.0)
+            quantise_x(1)
+            quantise_w(1, 0, 2, 4)
+            for j in range(n_slots + BACK_LAG):
+                if j == 1:
+                    regroup_w(1, 1, 0, 4, v_copy)
+                if j == 2:
+                    quantise_w(1, 1, 0, 4)
+                if j == 3:
+                    regroup_w(2, 0, 0, 4, v_copy)
+                if j == 4:
+                    quantise_w(2, 0, 0, 4)
+                if j == 6:
+                    regroup_w(2, 1, 0, 4, v_copy)
+                if j == 7:
+                    quantise_w(2, 1, 0, 4)
                 slot(j)

@@ -16,12 +16,12 @@ PACK = 4
 ROWS = 4096
 GROUPS = 2
 FEAT = 512
+ROW_TILES = 4
 HALF = 256
 
 SIZES = (512,) * 8
 X_BUFS = 16
-H_SPLIT = 384
-B2_LAG = 9
+B2_LAG = 10
 BACK_LAG = 13
 
 FLOPS = 2 * 2 * ROWS * GROUPS * FEAT * FEAT
@@ -46,10 +46,8 @@ def tile_blockresmlp_mixerblock_pb_t_kernel(tc, x_blocks, w1, b1, w2, b2, out):
         work = ctx.enter_context(tc.tile_pool(name="work", bufs=3))
         work2 = ctx.enter_context(tc.tile_pool(name="work2", bufs=2))
         out_pool = ctx.enter_context(tc.tile_pool(name="out", bufs=3))
-        psum_xt = ctx.enter_context(tc.psum_pool(name="psum_xt", bufs=1))
         psum_acc1 = ctx.enter_context(tc.psum_pool(name="psum_acc1", bufs=3))
-        psum_acc2 = ctx.enter_context(tc.psum_pool(name="psum_acc2", bufs=2))
-        psum_back = ctx.enter_context(tc.psum_pool(name="psum_back", bufs=2))
+        psum_short = ctx.enter_context(tc.psum_pool(name="psum_short", bufs=5))
 
         def piece_rows(dram, i):
             r0, rows, n = pieces[i]
@@ -99,6 +97,8 @@ def tile_blockresmlp_mixerblock_pb_t_kernel(tc, x_blocks, w1, b1, w2, b2, out):
 
         ident = keep.tile([P, P], F32)
         make_identity(nc, ident[:])
+        ident_bf = keep.tile([P, P], BF16)
+        make_identity(nc, ident_bf[:])
         b1_plus_1 = keep.tile([P, GROUPS, PACK], F32)
 
         w_codes = {}
@@ -116,6 +116,19 @@ def tile_blockresmlp_mixerblock_pb_t_kernel(tc, x_blocks, w1, b1, w2, b2, out):
                 out=w_grouped[layer, n][:, first:last],
                 in_=w_raw[layer, n][:].rearrange("p t (q s) -> p s q t", s=PACK)[:, first:last],
             )
+
+        def regroup_w_on_tensor(layer, n):
+            w_grouped[layer, n] = stage.tile([P, PACK, P, PACK], BF16, align_bytes=64, name="w_grouped")
+            for s in range(PACK):
+                bank = psum_short.tile([P, P, PACK], BF16, name="short")
+                nc.tensor.matmul(
+                    out=bank[:],
+                    lhsT=ident_bf[:],
+                    rhs=w_raw[layer, n][:].rearrange("p t (q s) -> p s q t", s=PACK)[:, s],
+                    start=True,
+                    stop=True,
+                )
+                nc.scalar.copy(out=w_grouped[layer, n][:, s], in_=bank[:])
 
         def quantise_w(layer, n, first, last):
             cols = slice(first * P, last * P)
@@ -140,7 +153,7 @@ def tile_blockresmlp_mixerblock_pb_t_kernel(tc, x_blocks, w1, b1, w2, b2, out):
 
         def transpose_x(i, half):
             words = x_sb[i][:].bitcast(F32)
-            bank = psum_xt.tile([P, 2, HALF], F32, name="xt")
+            bank = psum_short.tile([P, 2, HALF], F32, name="short")
             for k in range(2):
                 for u in range(2):
                     nc.tensor.transpose(
@@ -200,14 +213,19 @@ def tile_blockresmlp_mixerblock_pb_t_kernel(tc, x_blocks, w1, b1, w2, b2, out):
                 op1=ALU.max,
             )
 
-        def regroup_h(i, on_scalar):
+        def regroup_h(i, engine):
             if i not in grouped_h:
                 grouped_h[i] = work2.tile([P, n_rows(i), PACK], BF16, align_bytes=64, name="grouped_h")
-            rows = slice(H_SPLIT, n_rows(i)) if on_scalar else slice(0, H_SPLIT)
-            dst = grouped_h[i][:, rows, :].rearrange("p (c i) s -> p c s i", i=4)
-            src = elu_1[i][:, :, rows].rearrange("p s (c i) -> p c s i", i=4)
-            if on_scalar:
+            first, last = (0, 256) if engine is nc.vector else (256, 384) if engine is nc.gpsimd else (384, 512)
+            dst = grouped_h[i][:, first:last, :]
+            src = elu_1[i][:, :, first:last].rearrange("p s b -> p b s")
+            if engine is not nc.gpsimd:
+                dst = dst.rearrange("p (c i) s -> p c s i", i=4)
+                src = elu_1[i][:, :, first:last].rearrange("p s (c i) -> p c s i", i=4)
+            if engine is nc.scalar:
                 nc.scalar.activation(out=dst, in_=src, func=ACT.Copy, bias=-1.0, scale=1.0)
+            elif engine is nc.gpsimd:
+                nc.gpsimd.tensor_scalar(out=dst, in0=src, scalar1=1.0, scalar2=-1.0, op0=ALU.mult, op1=ALU.add)
             else:
                 nc.vector.tensor_scalar(out=dst, in0=src, scalar1=-1.0, scalar2=None, op0=ALU.add)
 
@@ -220,7 +238,7 @@ def tile_blockresmlp_mixerblock_pb_t_kernel(tc, x_blocks, w1, b1, w2, b2, out):
             h_q[i] = (codes, scales)
 
         def layer2(i, s):
-            acc2[i, s] = product(2, i, s, h_q[i], psum_acc2, "acc2")
+            acc2[i, s] = product(2, i, s, h_q[i], psum_short, "short")
 
         def add_b2(i, s):
             if s == 0:
@@ -229,7 +247,7 @@ def tile_blockresmlp_mixerblock_pb_t_kernel(tc, x_blocks, w1, b1, w2, b2, out):
             nc.scalar.activation(out=result_t[i][:, s, :], in_=acc2[i, s][:], func=ACT.Identity, bias=bias, scale=1.0)
 
         def transpose_back(i, r):
-            bank = psum_back.tile([P, PACK, P], F32, name="back")
+            bank = psum_short.tile([P, PACK, P], F32, name="short")
             for s in range(PACK):
                 nc.tensor.transpose(bank[:, s, :], result_t[i][:, s, r * P : (r + 1) * P], ident[:])
             back[i, r] = bank
@@ -243,8 +261,10 @@ def tile_blockresmlp_mixerblock_pb_t_kernel(tc, x_blocks, w1, b1, w2, b2, out):
                 in1=x_sb[i][:, r, :].rearrange("b (q s) -> b q s", s=PACK),
                 op=ALU.add,
             )
-            if r == n_rows(i) // P - 1:
-                nc.sync.dma_start(out=piece_rows(out, i), in_=out_sb[i][:])
+            per_store = 2 if i == n_pieces - 1 else ROW_TILES
+            if (r + 1) % per_store == 0:
+                done = slice(r + 1 - per_store, r + 1)
+                nc.sync.dma_start(out=piece_rows(out, i)[:, done, :], in_=out_sb[i][:, done, :])
 
         def is_piece(i):
             return 0 <= i < n_pieces
@@ -257,39 +277,41 @@ def tile_blockresmlp_mixerblock_pb_t_kernel(tc, x_blocks, w1, b1, w2, b2, out):
 
         def slot(j):
             i, k = divmod(j, PACK)
-            if is_piece(i):
+            if j < n_slots:
                 exponential(i, k)
-            if k % 2 == 1 and is_piece(i + 2):
-                regroup_x(i + 2, k // 2, nc.scalar.copy)
-            if 0 <= j - 1 < n_slots:
-                maximum(*divmod(j - 1, PACK))
-            if 0 <= j - BACK_LAG < n_slots:
-                transpose_back(*divmod(j - BACK_LAG, PACK))
-            if k == 3 and is_piece(i - 1):
-                quantise_h(i - 1)
             if 0 <= j - B2_LAG < n_slots:
                 add_b2(*divmod(j - B2_LAG, PACK))
-            if is_piece(i):
-                clamp(i, k)
-            if k % 2 == 0 and is_piece(i + 2):
-                transpose_x(i + 2, k // 2)
-            if is_piece((j + 1) // PACK):
-                layer1(*divmod(j + 1, PACK))
-            if k == 0 and is_piece(i + 1) and i >= 1:
-                quantise_x(i + 1)
-            if k == 1 and is_piece(i - 1):
-                regroup_h(i - 1, False)
             if 0 <= j + 1 - B2_LAG < n_slots:
                 layer2(*divmod(j + 1 - B2_LAG, PACK))
+            if 0 <= j - 1 < n_slots:
+                maximum(*divmod(j - 1, PACK))
+            if j + 1 < n_slots:
+                layer1(*divmod(j + 1, PACK))
+            if k == 3 and is_piece(i - 1):
+                quantise_h(i - 1)
+            if 0 <= j - BACK_LAG < n_slots:
+                transpose_back(*divmod(j - BACK_LAG, PACK))
+            if k % 2 == 0 and is_piece(i + 2):
+                transpose_x(i + 2, k // 2)
+            if k == 2 and is_piece(i - 1):
+                regroup_h(i - 1, nc.vector)
+            if k % 2 == 1 and is_piece(i + 2):
+                regroup_x(i + 2, k // 2, s_copy)
+            if k == 2 and is_piece(i - 1):
+                regroup_h(i - 1, nc.scalar)
+            if k == 0 and i >= 1 and is_piece(i + 1):
+                quantise_x(i + 1)
+            if j < n_slots:
+                clamp(i, k)
             if 0 <= j - BACK_LAG < n_slots:
                 finish(*divmod(j - BACK_LAG, PACK))
             if k == 1 and is_piece(i - 1):
-                regroup_h(i - 1, True)
+                regroup_h(i - 1, nc.gpsimd)
 
         with tc.manual_schedule(engines={mybir.EngineType.PE, mybir.EngineType.Activation, mybir.EngineType.DVE, mybir.EngineType.Pool}):
             v_copy, s_copy = nc.vector.tensor_copy, nc.scalar.copy
             for i in range(2):
-                for half in range(halves(i)):
+                for half in range(2):
                     transpose_x(i, half)
                     regroup_x(i, half, s_copy)
                 if i == 0:
@@ -307,12 +329,11 @@ def tile_blockresmlp_mixerblock_pb_t_kernel(tc, x_blocks, w1, b1, w2, b2, out):
                     regroup_w(1, 1, 0, 4, v_copy)
                 if j == 2:
                     quantise_w(1, 1, 0, 4)
+                    regroup_w_on_tensor(2, 0)
                 if j == 3:
-                    regroup_w(2, 0, 0, 4, v_copy)
-                if j == 4:
                     quantise_w(2, 0, 0, 4)
-                if j == 6:
-                    regroup_w(2, 1, 0, 4, v_copy)
-                if j == 7:
+                if j == 8:
+                    regroup_w_on_tensor(2, 1)
+                if j == 10:
                     quantise_w(2, 1, 0, 4)
                 slot(j)

@@ -248,6 +248,7 @@ def tile_blockresmlp_mixerblock_pb_t_kernel(tc, x_blocks, w1, b1, w2, b2, out):
 
         def transpose_back(i, r):
             bank = psum_short.tile([P, PACK, P], F32, name="short")
+            nc.tensor.matmul(out=bank[:, 0:2, :], lhsT=ident_bf[:], rhs=x_sb[i][:, r, 0:HALF], start=True, stop=True)
             for s in range(PACK):
                 nc.tensor.transpose(bank[:, s, :], result_t[i][:, s, r * P : (r + 1) * P], ident[:])
             back[i, r] = bank

@@ -10,60 +10,45 @@ U8 = mybir.dt.uint8
 FP8X4 = mybir.dt.float8_e4m3fn_x4
 ACT = mybir.ActivationFunctionType
 ALU = mybir.AluOpType
+ENGINE = mybir.EngineType
 
 P = 128
 PACK = 4
 ROWS = 4096
 GROUPS = 2
 FEAT = 512
-ROW_TILES = 4
-HALF = 256
-
-SIZES = (512,) * 8
-X_BUFS = 16
-B2_LAG = 10
-BACK_LAG = 13
+CHUNK = 512
+ROW_TILES = CHUNK // P
+HALF = CHUNK // 2
+N_PIECES = ROWS // CHUNK * GROUPS
+N_SLOTS = N_PIECES * PACK
 
 FLOPS = 2 * 2 * ROWS * GROUPS * FEAT * FEAT
 
 
 def tile_blockresmlp_mixerblock_pb_t_kernel(tc, x_blocks, w1, b1, w2, b2, out):
     nc = tc.nc
-    pieces = []
-    first_row = 0
-    for rows in SIZES:
-        for n in range(GROUPS):
-            pieces.append((first_row, rows, n))
-        first_row += rows
-    assert first_row == ROWS
-    n_pieces = len(pieces)
-    n_slots = PACK * n_pieces
-
     with ExitStack() as ctx:
         keep = ctx.enter_context(tc.tile_pool(name="keep", bufs=1))
         stage = ctx.enter_context(tc.tile_pool(name="stage", bufs=2))
-        x_pool = ctx.enter_context(tc.tile_pool(name="x", bufs=X_BUFS))
-        work = ctx.enter_context(tc.tile_pool(name="work", bufs=3))
+        x_pool = ctx.enter_context(tc.tile_pool(name="x", bufs=N_PIECES))
         work2 = ctx.enter_context(tc.tile_pool(name="work2", bufs=2))
-        out_pool = ctx.enter_context(tc.tile_pool(name="out", bufs=3))
-        psum_acc1 = ctx.enter_context(tc.psum_pool(name="psum_acc1", bufs=3))
-        psum_short = ctx.enter_context(tc.psum_pool(name="psum_short", bufs=5))
+        work3 = ctx.enter_context(tc.tile_pool(name="work3", bufs=3))
+        work4 = ctx.enter_context(tc.tile_pool(name="work4", bufs=6))
+        psum_layer1 = ctx.enter_context(tc.psum_pool(name="psum_layer1", bufs=3))
+        psum_layer2 = ctx.enter_context(tc.psum_pool(name="psum_layer2", bufs=2))
+        psum_turn = ctx.enter_context(tc.psum_pool(name="psum_turn", bufs=3))
 
-        def piece_rows(dram, i):
-            r0, rows, n = pieces[i]
-            return dram[r0 : r0 + rows, n * FEAT : (n + 1) * FEAT].rearrange("(p r) d -> p r d", p=P)
-
-        def n_rows(i):
-            return pieces[i][1]
-
-        def group(i):
-            return pieces[i][2]
+        def piece_of(dram, i):
+            c, n = divmod(i, GROUPS)
+            rows = dram[c * CHUNK : (c + 1) * CHUNK, n * FEAT : (n + 1) * FEAT]
+            return rows.rearrange("(p r) d -> p r d", r=ROW_TILES)
 
         x_sb = {}
 
         def load_x(i):
-            x_sb[i] = x_pool.tile([P, n_rows(i) // P, FEAT], BF16, name="x_sb")
-            nc.sync.dma_start(out=x_sb[i][:], in_=piece_rows(x_blocks, i))
+            x_sb[i] = x_pool.tile([P, ROW_TILES, FEAT], BF16, name="x_sb")
+            nc.sync.dma_start(out=x_sb[i][:], in_=piece_of(x_blocks, i))
 
         w_raw = {}
 
@@ -79,20 +64,20 @@ def tile_blockresmlp_mixerblock_pb_t_kernel(tc, x_blocks, w1, b1, w2, b2, out):
             nc.sync.dma_start(out=w_raw[2, n][:], in_=w2[n].rearrange("(p t) d -> p t d", t=PACK))
 
         def load_bias(dram, name):
-            as_given = keep.tile([P, GROUPS, PACK], BF16, name=name + "_bf16")
-            nc.scalar.dma_start(out=as_given[:], in_=dram.rearrange("g o (q s) -> q (g o) s", s=PACK))
-            return as_given
+            bias = keep.tile([P, GROUPS, PACK], BF16, name=name)
+            nc.scalar.dma_start(out=bias[:], in_=dram.rearrange("g o (q s) -> q (g o) s", s=PACK))
+            return bias
 
         load_x(0)
         load_w1(0)
-        b1_sb = load_bias(b1, "b1")
-        b2_sb = load_bias(b2, "b2")
+        b1_sb = load_bias(b1, "b1_sb")
+        b2_sb = load_bias(b2, "b2_sb")
         load_x(1)
         load_w1(1)
         load_w2(0)
         load_x(2)
         load_w2(1)
-        for i in range(3, n_pieces):
+        for i in range(3, N_PIECES):
             load_x(i)
 
         ident = keep.tile([P, P], F32)
@@ -101,33 +86,28 @@ def tile_blockresmlp_mixerblock_pb_t_kernel(tc, x_blocks, w1, b1, w2, b2, out):
         make_identity(nc, ident_bf[:])
         b1_plus_1 = keep.tile([P, GROUPS, PACK], F32)
 
+        w_grouped = {}
         w_codes = {}
         w_scales = {}
-        w_grouped = {}
         for layer in (1, 2):
             for n in range(GROUPS):
                 w_codes[layer, n] = keep.tile([P, FEAT], U32, align_bytes=64, name="w%d_%d_codes" % (layer, n))
                 w_scales[layer, n] = keep.tile([P, FEAT], U8, align_bytes=64, name="w%d_%d_scales" % (layer, n))
 
-        def regroup_w(layer, n, first, last, copy):
-            if (layer, n) not in w_grouped:
-                w_grouped[layer, n] = stage.tile([P, PACK, P, PACK], BF16, align_bytes=64, name="w_grouped")
-            copy(
-                out=w_grouped[layer, n][:, first:last],
-                in_=w_raw[layer, n][:].rearrange("p t (q s) -> p s q t", s=PACK)[:, first:last],
-            )
+        def w_slice(layer, n, s):
+            return w_raw[layer, n][:].rearrange("p t (q s) -> p s q t", s=PACK)[:, s]
+
+        def new_w_grouped(layer, n):
+            w_grouped[layer, n] = stage.tile([P, PACK, P, PACK], BF16, align_bytes=64, name="w_grouped")
+
+        def regroup_w_on_vector(layer, n, s):
+            nc.vector.tensor_copy(out=w_grouped[layer, n][:, s], in_=w_slice(layer, n, s))
 
         def regroup_w_on_tensor(layer, n):
-            w_grouped[layer, n] = stage.tile([P, PACK, P, PACK], BF16, align_bytes=64, name="w_grouped")
+            new_w_grouped(layer, n)
             for s in range(PACK):
-                bank = psum_short.tile([P, P, PACK], BF16, name="short")
-                nc.tensor.matmul(
-                    out=bank[:],
-                    lhsT=ident_bf[:],
-                    rhs=w_raw[layer, n][:].rearrange("p t (q s) -> p s q t", s=PACK)[:, s],
-                    start=True,
-                    stop=True,
-                )
+                bank = psum_turn.tile([P, P, PACK], BF16, name="turn")
+                nc.tensor.matmul(out=bank[:], lhsT=ident_bf[:], rhs=w_slice(layer, n, s), start=True, stop=True)
                 nc.scalar.copy(out=w_grouped[layer, n][:, s], in_=bank[:])
 
         def quantise_w(layer, n, first, last):
@@ -140,20 +120,32 @@ def tile_blockresmlp_mixerblock_pb_t_kernel(tc, x_blocks, w1, b1, w2, b2, out):
 
         xt = {}
         grouped_x = {}
-        x_q = {}
+        grouped_h = {}
+        x_operand = {}
         acc1 = {}
         exp_v = {}
-        elu_1 = {}
-        grouped_h = {}
-        h_q = {}
+        elu_plus_1 = {}
+        h_operand = {}
         acc2 = {}
         result_t = {}
         back = {}
         out_sb = {}
 
+        def quantise(grouped):
+            codes = work4.tile([P, CHUNK], U32, align_bytes=64, name="codes")
+            scales = work4.tile([P, CHUNK], U8, align_bytes=64, name="scales")
+            nc.vector.quantize_mx(out=codes[:].bitcast(FP8X4), scales=scales[:], in_=grouped[:])
+            return codes[:], scales[:]
+
+        def quantise_x(i):
+            x_operand[i] = quantise(grouped_x[i])
+
+        def quantise_h(i):
+            h_operand[i] = quantise(grouped_h[i])
+
         def transpose_x(i, half):
             words = x_sb[i][:].bitcast(F32)
-            bank = psum_short.tile([P, 2, HALF], F32, name="short")
+            bank = psum_turn.tile([P, 2, HALF], F32, name="turn")
             for k in range(2):
                 for u in range(2):
                     nc.tensor.transpose(
@@ -161,40 +153,39 @@ def tile_blockresmlp_mixerblock_pb_t_kernel(tc, x_blocks, w1, b1, w2, b2, out):
                     )
             xt[i, half] = bank
 
-        def regroup_x(i, half, copy):
+        def regroup_x(i, half):
             if half == 0:
-                grouped_x[i] = work.tile([P, n_rows(i) * PACK], BF16, align_bytes=64, name="grouped_x")
+                grouped_x[i] = work3.tile([P, CHUNK * PACK], BF16, align_bytes=64, name="grouped_x")
             pairs = grouped_x[i][:].bitcast(F32).rearrange("p (b u) -> p b u", u=2)
-            copy(out=pairs[:, half * HALF : (half + 1) * HALF, :], in_=xt[i, half][:].rearrange("p u b -> p b u"))
+            nc.scalar.copy(
+                out=pairs[:, half * HALF : (half + 1) * HALF, :], in_=xt[i, half][:].rearrange("p u b -> p b u")
+            )
 
-        def quantise_x(i):
-            codes = work.tile([P, n_rows(i)], U32, align_bytes=64, name="x_codes")
-            scales = work.tile([P, n_rows(i)], U8, align_bytes=64, name="x_scales")
-            nc.vector.quantize_mx(out=codes[:].bitcast(FP8X4), scales=scales[:], in_=grouped_x[i][:])
-            x_q[i] = (codes, scales)
-
-        def product(layer, i, s, operand, pool, name):
-            n = group(i)
+        def product(layer, i, s, operand, bank):
+            n = i % GROUPS
             codes, scales = operand
-            bank = pool.tile([P, n_rows(i)], F32, name=name)
             nc.tensor.matmul_mx(
                 out=bank[:],
                 lhsT=w_codes[layer, n][:, s * P : (s + 1) * P].bitcast(FP8X4),
                 lhsT_scale=w_scales[layer, n][:, s * P : (s + 1) * P],
-                rhs=codes[:].bitcast(FP8X4),
-                rhs_scale=scales[:],
+                rhs=codes.bitcast(FP8X4),
+                rhs_scale=scales,
                 start=True,
                 stop=True,
             )
             return bank
 
         def layer1(i, s):
-            acc1[i, s] = product(1, i, s, x_q[i], psum_acc1, "acc1")
+            if i < 2 and s % 2 == 1:
+                bank = psum_layer2.tile([P, CHUNK], F32, name="acc2")
+            else:
+                bank = psum_layer1.tile([P, CHUNK], F32, name="acc1")
+            acc1[i, s] = product(1, i, s, x_operand[i], bank)
 
         def exponential(i, s):
             if s == 0:
-                exp_v[i] = work.tile([P, PACK, n_rows(i)], F32, name="exp_v")
-            bias = b1_sb[:, group(i), s : s + 1]
+                exp_v[i] = work3.tile([P, PACK, CHUNK], F32, name="exp_v")
+            bias = b1_sb[:, i % GROUPS, s : s + 1]
             nc.scalar.activation(out=exp_v[i][:, s, :], in_=acc1[i, s][:], func=ACT.Exp, bias=bias, scale=1.0)
 
         def clamp(i, s):
@@ -203,51 +194,59 @@ def tile_blockresmlp_mixerblock_pb_t_kernel(tc, x_blocks, w1, b1, w2, b2, out):
 
         def maximum(i, s):
             if s == 0:
-                elu_1[i] = work2.tile([P, PACK, n_rows(i)], F32, name="elu_1")
+                elu_plus_1[i] = work2.tile([P, PACK, CHUNK], F32, name="elu_plus_1")
             nc.vector.scalar_tensor_tensor(
-                out=elu_1[i][:, s, :],
+                out=elu_plus_1[i][:, s, :],
                 in0=acc1[i, s][:],
-                scalar=b1_plus_1[:, group(i), s : s + 1],
+                scalar=b1_plus_1[:, i % GROUPS, s : s + 1],
                 in1=exp_v[i][:, s, :],
                 op0=ALU.add,
                 op1=ALU.max,
             )
 
-        def regroup_h(i, engine):
+        def last_pass_views(i, first, last):
             if i not in grouped_h:
-                grouped_h[i] = work2.tile([P, n_rows(i), PACK], BF16, align_bytes=64, name="grouped_h")
-            first, last = (0, 256) if engine is nc.vector else (256, 384) if engine is nc.gpsimd else (384, 512)
-            dst = grouped_h[i][:, first:last, :]
-            src = elu_1[i][:, :, first:last].rearrange("p s b -> p b s")
-            if engine is not nc.gpsimd:
-                dst = dst.rearrange("p (c i) s -> p c s i", i=4)
-                src = elu_1[i][:, :, first:last].rearrange("p s (c i) -> p c s i", i=4)
-            if engine is nc.scalar:
-                nc.scalar.activation(out=dst, in_=src, func=ACT.Copy, bias=-1.0, scale=1.0)
-            elif engine is nc.gpsimd:
-                nc.gpsimd.tensor_scalar(out=dst, in0=src, scalar1=1.0, scalar2=-1.0, op0=ALU.mult, op1=ALU.add)
-            else:
-                nc.vector.tensor_scalar(out=dst, in0=src, scalar1=-1.0, scalar2=None, op0=ALU.add)
+                grouped_h[i] = work2.tile([P, CHUNK * PACK], BF16, align_bytes=64, name="grouped_h")
+            h = grouped_h[i][:].rearrange("p (b s) -> p b s", s=PACK)[:, first:last, :]
+            return h, elu_plus_1[i][:, :, first:last]
 
-        def quantise_h(i):
-            codes = work.tile([P, n_rows(i)], U32, align_bytes=64, name="h_codes")
-            scales = work.tile([P, n_rows(i)], U8, align_bytes=64, name="h_scales")
-            nc.vector.quantize_mx(
-                out=codes[:].bitcast(FP8X4), scales=scales[:], in_=grouped_h[i][:].rearrange("p b s -> p (b s)")
+        def last_pass_on_vector(i, first, last):
+            h, e = last_pass_views(i, first, last)
+            nc.vector.tensor_scalar(
+                out=h.rearrange("p (c i) s -> p c s i", i=4),
+                in0=e.rearrange("p s (c i) -> p c s i", i=4),
+                scalar1=-1.0,
+                scalar2=None,
+                op0=ALU.add,
             )
-            h_q[i] = (codes, scales)
+
+        def last_pass_on_scalar(i, first, last):
+            h, e = last_pass_views(i, first, last)
+            nc.scalar.activation(
+                out=h.rearrange("p (c i) s -> p c s i", i=4),
+                in_=e.rearrange("p s (c i) -> p c s i", i=4),
+                func=ACT.Copy,
+                bias=-1.0,
+                scale=1.0,
+            )
+
+        def last_pass_on_gpsimd(i, first, last):
+            h, e = last_pass_views(i, first, last)
+            nc.gpsimd.tensor_scalar(
+                out=h, in0=e.rearrange("p s b -> p b s"), scalar1=1.0, scalar2=-1.0, op0=ALU.mult, op1=ALU.add
+            )
 
         def layer2(i, s):
-            acc2[i, s] = product(2, i, s, h_q[i], psum_short, "short")
+            acc2[i, s] = product(2, i, s, h_operand[i], psum_layer2.tile([P, CHUNK], F32, name="acc2"))
 
         def add_b2(i, s):
             if s == 0:
-                result_t[i] = work.tile([P, PACK, n_rows(i)], F32, name="result_t")
-            bias = b2_sb[:, group(i), s : s + 1]
+                result_t[i] = work3.tile([P, PACK, CHUNK], F32, name="result_t")
+            bias = b2_sb[:, i % GROUPS, s : s + 1]
             nc.scalar.activation(out=result_t[i][:, s, :], in_=acc2[i, s][:], func=ACT.Identity, bias=bias, scale=1.0)
 
         def transpose_back(i, r):
-            bank = psum_short.tile([P, PACK, P], F32, name="short")
+            bank = psum_turn.tile([P, PACK, P], F32, name="turn")
             nc.tensor.matmul(out=bank[:, 0:2, :], lhsT=ident_bf[:], rhs=x_sb[i][:, r, 0:HALF], start=True, stop=True)
             for s in range(PACK):
                 nc.tensor.transpose(bank[:, s, :], result_t[i][:, s, r * P : (r + 1) * P], ident[:])
@@ -255,86 +254,86 @@ def tile_blockresmlp_mixerblock_pb_t_kernel(tc, x_blocks, w1, b1, w2, b2, out):
 
         def finish(i, r):
             if r == 0:
-                out_sb[i] = out_pool.tile([P, n_rows(i) // P, FEAT], F32, name="out_sb")
+                out_sb[i] = work3.tile([P, ROW_TILES, FEAT], F32, name="out_sb")
             nc.vector.tensor_tensor(
                 out=out_sb[i][:, r, :].rearrange("b (q s) -> b q s", s=PACK),
                 in0=back[i, r][:].rearrange("b s q -> b q s"),
                 in1=x_sb[i][:, r, :].rearrange("b (q s) -> b q s", s=PACK),
                 op=ALU.add,
             )
-            per_store = 2 if i == n_pieces - 1 else ROW_TILES
+            per_store = 2 if i == N_PIECES - 1 else ROW_TILES
             if (r + 1) % per_store == 0:
-                done = slice(r + 1 - per_store, r + 1)
-                nc.sync.dma_start(out=piece_rows(out, i)[:, done, :], in_=out_sb[i][:, done, :])
+                ready = slice(r + 1 - per_store, r + 1)
+                nc.sync.dma_start(out=piece_of(out, i)[:, ready, :], in_=out_sb[i][:, ready, :])
 
         def is_piece(i):
-            return 0 <= i < n_pieces
+            return 0 <= i < N_PIECES
 
-        def halves(i):
-            return n_rows(i) // HALF if is_piece(i) else 0
-
-        def tiles(i):
-            return n_rows(i) // P if is_piece(i) else 0
+        def at(stage_of_slice, slot):
+            if 0 <= slot < N_SLOTS:
+                stage_of_slice(*divmod(slot, PACK))
 
         def slot(j):
             i, k = divmod(j, PACK)
-            if j < n_slots:
-                exponential(i, k)
-            if 0 <= j - B2_LAG < n_slots:
-                add_b2(*divmod(j - B2_LAG, PACK))
-            if 0 <= j + 1 - B2_LAG < n_slots:
-                layer2(*divmod(j + 1 - B2_LAG, PACK))
-            if 0 <= j - 1 < n_slots:
-                maximum(*divmod(j - 1, PACK))
-            if j + 1 < n_slots:
-                layer1(*divmod(j + 1, PACK))
+            at(layer2, j + 1 - B2_LAG)
             if k == 3 and is_piece(i - 1):
-                quantise_h(i - 1)
-            if 0 <= j - BACK_LAG < n_slots:
-                transpose_back(*divmod(j - BACK_LAG, PACK))
-            if k % 2 == 0 and is_piece(i + 2):
-                transpose_x(i + 2, k // 2)
+                last_pass_on_scalar(i - 1, 384, 512)
+            at(exponential, j)
+            at(add_b2, j - B2_LAG)
+            if j in weights:
+                weights[j]()
+            at(layer1, j + 1)
+            at(maximum, j - 1)
+            at(clamp, j)
             if k == 2 and is_piece(i - 1):
-                regroup_h(i - 1, nc.vector)
-            if k % 2 == 1 and is_piece(i + 2):
-                regroup_x(i + 2, k // 2, s_copy)
-            if k == 2 and is_piece(i - 1):
-                regroup_h(i - 1, nc.scalar)
+                last_pass_on_vector(i - 1, 0, 256)
+            at(transpose_back, j - BACK_LAG)
             if k == 0 and i >= 1 and is_piece(i + 1):
                 quantise_x(i + 1)
-            if j < n_slots:
-                clamp(i, k)
-            if 0 <= j - BACK_LAG < n_slots:
-                finish(*divmod(j - BACK_LAG, PACK))
+            if k % 2 == 1 and is_piece(i + 2):
+                regroup_x(i + 2, k // 2)
+            if k == 3 and is_piece(i - 1):
+                quantise_h(i - 1)
             if k == 1 and is_piece(i - 1):
-                regroup_h(i - 1, nc.gpsimd)
+                last_pass_on_gpsimd(i - 1, 256, 384)
+            if k % 2 == 0 and is_piece(i + 2):
+                transpose_x(i + 2, k // 2)
+            at(finish, j - BACK_LAG)
 
-        with tc.manual_schedule(engines={mybir.EngineType.PE, mybir.EngineType.Activation, mybir.EngineType.DVE, mybir.EngineType.Pool}):
-            v_copy, s_copy = nc.vector.tensor_copy, nc.scalar.copy
+        B2_LAG = 10
+        BACK_LAG = 13
+
+        def regroup_w11():
+            new_w_grouped(1, 1)
+            nc.vector.tensor_copy(
+                out=w_grouped[1, 1][:], in_=w_raw[1, 1][:].rearrange("p t (q s) -> p s q t", s=PACK)
+            )
+
+        weights = {
+            0: regroup_w11,
+            1: lambda: quantise_w(1, 1, 0, PACK),
+            2: lambda: regroup_w_on_tensor(2, 0),
+            3: lambda: quantise_w(2, 0, 0, PACK),
+            8: lambda: regroup_w_on_tensor(2, 1),
+            12: lambda: quantise_w(2, 1, 0, PACK),
+        }
+
+        with tc.manual_schedule(engines={ENGINE.PE, ENGINE.Activation, ENGINE.DVE, ENGINE.Pool}):
             for i in range(2):
                 for half in range(2):
                     transpose_x(i, half)
-                    regroup_x(i, half, s_copy)
+                    regroup_x(i, half)
                 if i == 0:
-                    regroup_w(1, 0, 0, 1, v_copy)
-                    regroup_w(1, 0, 1, 2, v_copy)
+                    new_w_grouped(1, 0)
+                    regroup_w_on_vector(1, 0, 0)
+                    regroup_w_on_vector(1, 0, 1)
                     quantise_w(1, 0, 0, 2)
                     quantise_x(0)
-            layer1(0, 0)
-            regroup_w(1, 0, 2, 4, v_copy)
+            at(layer1, 0)
+            regroup_w_on_vector(1, 0, 2)
+            regroup_w_on_vector(1, 0, 3)
             nc.vector.tensor_scalar_add(out=b1_plus_1[:], in0=b1_sb[:], scalar1=1.0)
             quantise_x(1)
-            quantise_w(1, 0, 2, 4)
-            for j in range(n_slots + BACK_LAG):
-                if j == 1:
-                    regroup_w(1, 1, 0, 4, v_copy)
-                if j == 2:
-                    quantise_w(1, 1, 0, 4)
-                    regroup_w_on_tensor(2, 0)
-                if j == 3:
-                    quantise_w(2, 0, 0, 4)
-                if j == 8:
-                    regroup_w_on_tensor(2, 1)
-                if j == 10:
-                    quantise_w(2, 1, 0, 4)
+            quantise_w(1, 0, 2, PACK)
+            for j in range(N_SLOTS + BACK_LAG):
                 slot(j)

@@ -86,6 +86,12 @@ def tile_blockresmlp_mixerblock_pb_t_kernel(tc, x_blocks, w1, b1, w2, b2, out):
         make_identity(nc, ident_bf[:])
         b1_plus_1 = keep.tile([P, GROUPS, PACK], F32)
 
+        zeros = keep.tile([P, CHUNK], BF16)
+        nc.vector.memset(zeros[:], 0.0)
+
+        def keep_busy(bank):
+            nc.tensor.matmul(out=bank[:], lhsT=zeros[:, 0:P], rhs=zeros[:], start=True, stop=True)
+
         w_grouped = {}
         w_codes = {}
         w_scales = {}
@@ -237,7 +243,11 @@ def tile_blockresmlp_mixerblock_pb_t_kernel(tc, x_blocks, w1, b1, w2, b2, out):
             )
 
         def layer2(i, s):
-            acc2[i, s] = product(2, i, s, h_operand[i], psum_layer2.tile([P, CHUNK], F32, name="acc2"))
+            if i >= N_PIECES - 2 and s % 2 == 1:
+                bank = psum_layer1.tile([P, CHUNK], F32, name="acc1")
+            else:
+                bank = psum_layer2.tile([P, CHUNK], F32, name="acc2")
+            acc2[i, s] = product(2, i, s, h_operand[i], bank)
 
         def add_b2(i, s):
             if s == 0:
@@ -275,23 +285,27 @@ def tile_blockresmlp_mixerblock_pb_t_kernel(tc, x_blocks, w1, b1, w2, b2, out):
 
         def slot(j):
             i, k = divmod(j, PACK)
-            at(layer2, j + 1 - B2_LAG)
+            if j == N_SLOTS - PACK + B2_LAG:
+                for s in range(PACK):
+                    layer2(N_PIECES - 1, s)
+            elif j + 1 - B2_LAG < N_SLOTS - PACK:
+                at(layer2, j + 1 - B2_LAG)
             if k == 3 and is_piece(i - 1):
                 last_pass_on_scalar(i - 1, 384, 512)
             at(exponential, j)
             at(add_b2, j - B2_LAG)
+            if k % 2 == 1 and is_piece(i + 2):
+                regroup_x(i + 2, k // 2)
             if j in weights:
                 weights[j]()
             at(layer1, j + 1)
+            at(transpose_back, j - BACK_LAG)
             at(maximum, j - 1)
             at(clamp, j)
             if k == 2 and is_piece(i - 1):
                 last_pass_on_vector(i - 1, 0, 256)
-            at(transpose_back, j - BACK_LAG)
             if k == 0 and i >= 1 and is_piece(i + 1):
                 quantise_x(i + 1)
-            if k % 2 == 1 and is_piece(i + 2):
-                regroup_x(i + 2, k // 2)
             if k == 3 and is_piece(i - 1):
                 quantise_h(i - 1)
             if k == 1 and is_piece(i - 1):
@@ -312,13 +326,16 @@ def tile_blockresmlp_mixerblock_pb_t_kernel(tc, x_blocks, w1, b1, w2, b2, out):
         weights = {
             0: regroup_w11,
             1: lambda: quantise_w(1, 1, 0, PACK),
-            2: lambda: regroup_w_on_tensor(2, 0),
-            3: lambda: quantise_w(2, 0, 0, PACK),
+            3: lambda: regroup_w_on_tensor(2, 0),
+            4: lambda: quantise_w(2, 0, 0, PACK),
             8: lambda: regroup_w_on_tensor(2, 1),
             12: lambda: quantise_w(2, 1, 0, PACK),
         }
 
         with tc.manual_schedule(engines={ENGINE.PE, ENGINE.Activation, ENGINE.DVE, ENGINE.Pool}):
+            warm_up = psum_turn.tile([P, CHUNK], F32, name="turn")
+            for k in range(4):
+                keep_busy(warm_up)
             for i in range(2):
                 for half in range(2):
                     transpose_x(i, half)

from contextlib import ExitStack

import concourse.mybir as mybir
from concourse.masks import make_identity

F32 = mybir.dt.float32
BF16 = mybir.dt.bfloat16
U32 = mybir.dt.uint32
U8 = mybir.dt.uint8
FP8X4 = mybir.dt.float8_e4m3fn_x4
ACT = mybir.ActivationFunctionType
ALU = mybir.AluOpType
ENGINE = mybir.EngineType

P = 128
PACK = 4
ROWS = 4096
GROUPS = 2
FEAT = 512
CHUNK = 512
ROW_TILES = CHUNK // P
HALF = CHUNK // 2
N_PIECES = ROWS // CHUNK * GROUPS
N_SLOTS = N_PIECES * PACK

FLOPS = 2 * 2 * ROWS * GROUPS * FEAT * FEAT


def tile_blockresmlp_mixerblock_pb_t_kernel(tc, x_blocks, w1, b1, w2, b2, out):
    nc = tc.nc
    with ExitStack() as ctx:
        keep = ctx.enter_context(tc.tile_pool(name="keep", bufs=1))
        stage = ctx.enter_context(tc.tile_pool(name="stage", bufs=2))
        x_pool = ctx.enter_context(tc.tile_pool(name="x", bufs=N_PIECES))
        work2 = ctx.enter_context(tc.tile_pool(name="work2", bufs=2))
        work3 = ctx.enter_context(tc.tile_pool(name="work3", bufs=3))
        work4 = ctx.enter_context(tc.tile_pool(name="work4", bufs=6))
        psum_layer1 = ctx.enter_context(tc.psum_pool(name="psum_layer1", bufs=3))
        psum_layer2 = ctx.enter_context(tc.psum_pool(name="psum_layer2", bufs=2))
        psum_turn = ctx.enter_context(tc.psum_pool(name="psum_turn", bufs=3))

        def piece_of(dram, i):
            c, n = divmod(i, GROUPS)
            rows = dram[c * CHUNK : (c + 1) * CHUNK, n * FEAT : (n + 1) * FEAT]
            return rows.rearrange("(p r) d -> p r d", r=ROW_TILES)

        x_sb = {}

        def load_x(i):
            x_sb[i] = x_pool.tile([P, ROW_TILES, FEAT], BF16, name="x_sb")
            nc.sync.dma_start(out=x_sb[i][:], in_=piece_of(x_blocks, i))

        w_raw = {}

        def load_w1(n):
            w_raw[1, n] = stage.tile([P, PACK, FEAT], BF16, name="w1_raw")
            nc.sync.dma_start(
                out=w_raw[1, n][:].rearrange("p (u e) h -> p u (e h)", e=2),
                in_=w1[n].rearrange("(u p e) h -> p u (e h)", u=2, e=2),
            )

        def load_w2(n):
            w_raw[2, n] = stage.tile([P, PACK, FEAT], BF16, name="w2_raw")
            nc.sync.dma_start(out=w_raw[2, n][:], in_=w2[n].rearrange("(p t) d -> p t d", t=PACK))

        def load_bias(dram, name):
            bias = keep.tile([P, GROUPS, PACK], BF16, name=name)
            nc.scalar.dma_start(out=bias[:], in_=dram.rearrange("g o (q s) -> q (g o) s", s=PACK))
            return bias

        load_x(0)
        load_w1(0)
        b1_sb = load_bias(b1, "b1_sb")
        b2_sb = load_bias(b2, "b2_sb")
        load_x(1)
        load_w1(1)
        load_w2(0)
        load_x(2)
        load_w2(1)
        for i in range(3, N_PIECES):
            load_x(i)

        ident = keep.tile([P, P], F32)
        make_identity(nc, ident[:])
        ident_bf = keep.tile([P, P], BF16)
        make_identity(nc, ident_bf[:])
        b1_plus_1 = keep.tile([P, GROUPS, PACK], F32)

        zeros = keep.tile([P, CHUNK], BF16)
        nc.vector.memset(zeros[:], 0.0)

        def keep_busy(bank):
            nc.tensor.matmul(out=bank[:], lhsT=zeros[:, 0:P], rhs=zeros[:], start=True, stop=True)

        w_grouped = {}
        w_codes = {}
        w_scales = {}
        for layer in (1, 2):
            for n in range(GROUPS):
                w_codes[layer, n] = keep.tile([P, FEAT], U32, align_bytes=64, name="w%d_%d_codes" % (layer, n))
                w_scales[layer, n] = keep.tile([P, FEAT], U8, align_bytes=64, name="w%d_%d_scales" % (layer, n))

        def w_slice(layer, n, s):
            return w_raw[layer, n][:].rearrange("p t (q s) -> p s q t", s=PACK)[:, s]

        def new_w_grouped(layer, n):
            w_grouped[layer, n] = stage.tile([P, PACK, P, PACK], BF16, align_bytes=64, name="w_grouped")

        def regroup_w_on_vector(layer, n, s):
            nc.vector.tensor_copy(out=w_grouped[layer, n][:, s], in_=w_slice(layer, n, s))

        def regroup_w_on_tensor(layer, n):
            new_w_grouped(layer, n)
            for s in range(PACK):
                bank = psum_turn.tile([P, P, PACK], BF16, name="turn")
                nc.tensor.matmul(out=bank[:], lhsT=ident_bf[:], rhs=w_slice(layer, n, s), start=True, stop=True)
                nc.scalar.copy(out=w_grouped[layer, n][:, s], in_=bank[:])

        def quantise_w(layer, n, first, last):
            cols = slice(first * P, last * P)
            nc.vector.quantize_mx(
                out=w_codes[layer, n][:, cols].bitcast(FP8X4),
                scales=w_scales[layer, n][:, cols],
                in_=w_grouped[layer, n][:, first:last].rearrange("p s q t -> p (s q t)"),
            )

        xt = {}
        grouped_x = {}
        grouped_h = {}
        x_operand = {}
        acc1 = {}
        exp_v = {}
        elu_plus_1 = {}
        h_operand = {}
        acc2 = {}
        result_t = {}
        back = {}
        out_sb = {}

        def quantise(grouped):
            codes = work4.tile([P, CHUNK], U32, align_bytes=64, name="codes")
            scales = work4.tile([P, CHUNK], U8, align_bytes=64, name="scales")
            nc.vector.quantize_mx(out=codes[:].bitcast(FP8X4), scales=scales[:], in_=grouped[:])
            return codes[:], scales[:]

        def quantise_x(i):
            x_operand[i] = quantise(grouped_x[i])

        def quantise_h(i):
            h_operand[i] = quantise(grouped_h[i])

        def transpose_x(i, half):
            words = x_sb[i][:].bitcast(F32)
            bank = psum_turn.tile([P, 2, HALF], F32, name="turn")
            for k in range(2):
                for u in range(2):
                    nc.tensor.transpose(
                        bank[:, u, k * P : (k + 1) * P], words[:, 2 * half + k, u * P : (u + 1) * P], ident[:]
                    )
            xt[i, half] = bank

        def regroup_x(i, half):
            if half == 0:
                grouped_x[i] = work3.tile([P, CHUNK * PACK], BF16, align_bytes=64, name="grouped_x")
            pairs = grouped_x[i][:].bitcast(F32).rearrange("p (b u) -> p b u", u=2)
            nc.scalar.copy(
                out=pairs[:, half * HALF : (half + 1) * HALF, :], in_=xt[i, half][:].rearrange("p u b -> p b u")
            )

        def product(layer, i, s, operand, bank):
            n = i % GROUPS
            codes, scales = operand
            nc.tensor.matmul_mx(
                out=bank[:],
                lhsT=w_codes[layer, n][:, s * P : (s + 1) * P].bitcast(FP8X4),
                lhsT_scale=w_scales[layer, n][:, s * P : (s + 1) * P],
                rhs=codes.bitcast(FP8X4),
                rhs_scale=scales,
                start=True,
                stop=True,
            )
            return bank

        def layer1(i, s):
            if i < 2 and s % 2 == 1:
                bank = psum_layer2.tile([P, CHUNK], F32, name="acc2")
            else:
                bank = psum_layer1.tile([P, CHUNK], F32, name="acc1")
            acc1[i, s] = product(1, i, s, x_operand[i], bank)

        def exponential(i, s):
            if s == 0:
                exp_v[i] = work3.tile([P, PACK, CHUNK], F32, name="exp_v")
            bias = b1_sb[:, i % GROUPS, s : s + 1]
            nc.scalar.activation(out=exp_v[i][:, s, :], in_=acc1[i, s][:], func=ACT.Exp, bias=bias, scale=1.0)

        def clamp(i, s):
            e = exp_v[i][:, s, :]
            nc.gpsimd.tensor_scalar(out=e, in0=e, scalar1=1.0, scalar2=0.0, op0=ALU.min, op1=ALU.max)

        def maximum(i, s):
            if s == 0:
                elu_plus_1[i] = work2.tile([P, PACK, CHUNK], F32, name="elu_plus_1")
            nc.vector.scalar_tensor_tensor(
                out=elu_plus_1[i][:, s, :],
                in0=acc1[i, s][:],
                scalar=b1_plus_1[:, i % GROUPS, s : s + 1],
                in1=exp_v[i][:, s, :],
                op0=ALU.add,
                op1=ALU.max,
            )

        def last_pass_views(i, first, last):
            if i not in grouped_h:
                grouped_h[i] = work2.tile([P, CHUNK * PACK], BF16, align_bytes=64, name="grouped_h")
            h = grouped_h[i][:].rearrange("p (b s) -> p b s", s=PACK)[:, first:last, :]
            return h, elu_plus_1[i][:, :, first:last]

        def last_pass_on_vector(i, first, last):
            h, e = last_pass_views(i, first, last)
            nc.vector.tensor_scalar(
                out=h.rearrange("p (c i) s -> p c s i", i=4),
                in0=e.rearrange("p s (c i) -> p c s i", i=4),
                scalar1=-1.0,
                scalar2=None,
                op0=ALU.add,
            )

        def last_pass_on_scalar(i, first, last):
            h, e = last_pass_views(i, first, last)
            nc.scalar.activation(
                out=h.rearrange("p (c i) s -> p c s i", i=4),
                in_=e.rearrange("p s (c i) -> p c s i", i=4),
                func=ACT.Copy,
                bias=-1.0,
                scale=1.0,
            )

        def last_pass_on_gpsimd(i, first, last):
            h, e = last_pass_views(i, first, last)
            nc.gpsimd.tensor_scalar(
                out=h, in0=e.rearrange("p s b -> p b s"), scalar1=1.0, scalar2=-1.0, op0=ALU.mult, op1=ALU.add
            )

        def layer2(i, s):
            if i >= N_PIECES - 2 and s % 2 == 1:
                bank = psum_layer1.tile([P, CHUNK], F32, name="acc1")
            else:
                bank = psum_layer2.tile([P, CHUNK], F32, name="acc2")
            acc2[i, s] = product(2, i, s, h_operand[i], bank)

        def add_b2(i, s):
            if s == 0:
                result_t[i] = work3.tile([P, PACK, CHUNK], F32, name="result_t")
            bias = b2_sb[:, i % GROUPS, s : s + 1]
            nc.scalar.activation(out=result_t[i][:, s, :], in_=acc2[i, s][:], func=ACT.Identity, bias=bias, scale=1.0)

        def transpose_back(i, r):
            bank = psum_turn.tile([P, PACK, P], F32, name="turn")
            nc.tensor.matmul(out=bank[:, 0:2, :], lhsT=ident_bf[:], rhs=x_sb[i][:, r, 0:HALF], start=True, stop=True)
            for s in range(PACK):
                nc.tensor.transpose(bank[:, s, :], result_t[i][:, s, r * P : (r + 1) * P], ident[:])
            back[i, r] = bank

        def finish(i, r):
            if r == 0:
                out_sb[i] = work3.tile([P, ROW_TILES, FEAT], F32, name="out_sb")
            nc.vector.tensor_tensor(
                out=out_sb[i][:, r, :].rearrange("b (q s) -> b q s", s=PACK),
                in0=back[i, r][:].rearrange("b s q -> b q s"),
                in1=x_sb[i][:, r, :].rearrange("b (q s) -> b q s", s=PACK),
                op=ALU.add,
            )
            per_store = 2 if i == N_PIECES - 1 else ROW_TILES
            if (r + 1) % per_store == 0:
                ready = slice(r + 1 - per_store, r + 1)
                nc.sync.dma_start(out=piece_of(out, i)[:, ready, :], in_=out_sb[i][:, ready, :])

        def is_piece(i):
            return 0 <= i < N_PIECES

        def at(stage_of_slice, slot):
            if 0 <= slot < N_SLOTS:
                stage_of_slice(*divmod(slot, PACK))

        def slot(j):
            i, k = divmod(j, PACK)
            if j == N_SLOTS - PACK + B2_LAG:
                for s in range(PACK):
                    layer2(N_PIECES - 1, s)
            elif j + 1 - B2_LAG < N_SLOTS - PACK:
                at(layer2, j + 1 - B2_LAG)
            if k == 3 and is_piece(i - 1):
                last_pass_on_scalar(i - 1, 384, 512)
            at(exponential, j)
            at(add_b2, j - B2_LAG)
            if k % 2 == 1 and is_piece(i + 2):
                regroup_x(i + 2, k // 2)
            if j in weights:
                weights[j]()
            at(layer1, j + 1)
            at(transpose_back, j - BACK_LAG)
            at(maximum, j - 1)
            at(clamp, j)
            if k == 2 and is_piece(i - 1):
                last_pass_on_vector(i - 1, 0, 256)
            if k == 0 and i >= 1 and is_piece(i + 1):
                quantise_x(i + 1)
            if k == 3 and is_piece(i - 1):
                quantise_h(i - 1)
            if k == 1 and is_piece(i - 1):
                last_pass_on_gpsimd(i - 1, 256, 384)
            if k % 2 == 0 and is_piece(i + 2):
                transpose_x(i + 2, k // 2)
            at(finish, j - BACK_LAG)

        B2_LAG = 10
        BACK_LAG = 13

        def regroup_w11():
            new_w_grouped(1, 1)
            nc.vector.tensor_copy(
                out=w_grouped[1, 1][:], in_=w_raw[1, 1][:].rearrange("p t (q s) -> p s q t", s=PACK)
            )

        weights = {
            0: regroup_w11,
            1: lambda: quantise_w(1, 1, 0, PACK),
            3: lambda: regroup_w_on_tensor(2, 0),
            4: lambda: quantise_w(2, 0, 0, PACK),
            8: lambda: regroup_w_on_tensor(2, 1),
            12: lambda: quantise_w(2, 1, 0, PACK),
        }

        with tc.manual_schedule(engines={ENGINE.PE, ENGINE.Activation, ENGINE.DVE, ENGINE.Pool}):
            warm_up = psum_turn.tile([P, CHUNK], F32, name="turn")
            for k in range(4):
                keep_busy(warm_up)
            for i in range(2):
                for half in range(2):
                    transpose_x(i, half)
                    regroup_x(i, half)
                if i == 0:
                    new_w_grouped(1, 0)
                    regroup_w_on_vector(1, 0, 0)
                    regroup_w_on_vector(1, 0, 1)
                    quantise_w(1, 0, 0, 2)
                    quantise_x(0)
            at(layer1, 0)
            regroup_w_on_vector(1, 0, 2)
            regroup_w_on_vector(1, 0, 3)
            nc.vector.tensor_scalar_add(out=b1_plus_1[:], in0=b1_sb[:], scalar1=1.0)
            quantise_x(1)
            quantise_w(1, 0, 2, PACK)
            for j in range(N_SLOTS + BACK_LAG):
                slot(j)
